import numpy as np
import ml_dtypes


def mxq(x, axis, fmt="e4m3"):
    dtype, down = {"e4m3": (ml_dtypes.float8_e4m3fn, 7), "e5m2": (ml_dtypes.float8_e5m2, 14)}[fmt]
    v = np.moveaxis(np.asarray(x, np.float32).astype(ml_dtypes.bfloat16).astype(np.float64), axis, -1)
    blocks = v.reshape(v.shape[:-1] + (-1, 32))
    amax = np.abs(blocks).max(-1, keepdims=True)
    byte = np.maximum(np.where(amax > 0, np.frexp(amax)[1] - 1 + 127, 0) - down, 1)
    scale = np.exp2(byte - 127.0)
    codes = (blocks / scale).astype(np.float32).astype(dtype).astype(np.float64)
    return np.moveaxis((codes * scale).reshape(v.shape), -1, axis)


WIDE = False


def mx_kscale(k):
    if not WIDE:
        return np.ones(k)
    levels = np.array([10, -10, 5, -5, 0])
    a = np.random.permutation(np.resize(levels, k // 512 * 4)).reshape(k // 512, 4)
    idx = np.arange(k)
    return np.exp2(a[idx // 512, idx % 128 // 32])


BF16 = ml_dtypes.bfloat16


def bf(x):
    return np.asarray(x, np.float32).astype(BF16)


def f64(x):
    return np.asarray(x).astype(np.float64)


B, T, F, N, SR, GROUPS = 1, 64, 65537, 64, 2048, ((0, 256, 16), (256, 512, 32), (512, 1024, 64))
EPS = 1e-8
TAGS = ('16', '32', '64')
R = (F - 1) * 2 // SR


def setup_inputs():
    lev = 10.0 ** np.random.uniform(-4.5, 0.0, (B, 1, T))
    inp = {'x_real': bf(lev * (np.random.standard_normal((B, F, T)) + 0.5 * np.random.standard_normal((B, 1, T)))),
           'x_imag': bf(lev * (np.random.standard_normal((B, F, T)) + 0.5 * np.random.standard_normal((B, 1, T)))),
           'sample_rate': SR}
    for (s0, e0, w0), tag in zip(GROUPS, TAGS):
        k = (e0 - s0) // w0
        ch = 2 * w0 * R
        s = mx_kscale(ch)
        inp['g' + tag] = bf(np.random.uniform(0.5, 1.5, (k, ch)) * s)
        inp['b' + tag] = bf(0.1 * np.random.standard_normal((k, ch)) * s)
        inp['W' + tag] = bf(np.random.standard_normal((k, ch, N)) / np.sqrt(ch) / s[:, None])
        inp['c' + tag] = bf(0.1 * np.random.standard_normal((k, N)))
    return inp


def _band_group(x_real, x_imag, s, e, w, g, b, W, c):
    nb, _, nt = x_real.shape
    k = (e - s) // w
    xr = x_real[:, s:e, :].reshape(nb, k, w, nt)
    xi = x_imag[:, s:e, :].reshape(nb, k, w, nt)
    X = np.concatenate([xr, xi], axis=2)
    mu = X.mean(axis=2, keepdims=True)
    var = X.var(axis=2, keepdims=True)
    Xn = (X - mu) / np.sqrt(var + EPS)
    Xn = Xn * g[None, :, :, None] + b[None, :, :, None]
    Xq = mxq(Xn, 2, 'e4m3')
    Wq = mxq(W, 1, 'e4m3')
    y = Xq.transpose(0, 1, 3, 2) @ Wq[None]
    return y.transpose(0, 2, 1, 3) + c[None, None, :, :]


def reference(x_real, x_imag, sample_rate, g16, b16, W16, c16, g32, b32, W32, c32, g64, b64, W64, c64):
    x_real, x_imag = f64(x_real), f64(x_imag)
    nf = x_real.shape[1]
    n_fft = (nf - 1) * 2
    sr = int(sample_rate)
    params = [(g16, b16, W16, c16), (g32, b32, W32, c32), (g64, b64, W64, c64)]
    feats = []
    for (s, e, w), (g, b, W, c) in zip(GROUPS, params):
        sb = s * n_fft // sr
        eb = min(e * n_fft // sr, nf)
        wb = w * n_fft // sr
        feats.append(_band_group(x_real, x_imag, sb, eb, wb, f64(g), f64(b), f64(W), f64(c)))
    out = np.concatenate(feats, axis=2)
    return np.transpose(out, (0, 3, 2, 1))

@@ -1,0 +1,460 @@
+from contextlib import ExitStack
+
+import concourse.mybir as mybir
+from concourse.masks import make_identity
+
+F32 = mybir.dt.float32
+BF16 = mybir.dt.bfloat16
+U32 = mybir.dt.uint32
+U8 = mybir.dt.uint8
+FP8X4 = mybir.dt.float8_e4m3fn_x4
+ALU = mybir.AluOpType
+ACT = mybir.ActivationFunctionType
+AX = mybir.AxisListType
+
+P = 128
+T = 64
+N_OUT = 64
+PACK = 4
+K_PASS = P * PACK
+EPS = 1e-8
+
+GROUP_BINS = ((0, 16384, 1024), (16384, 32768, 2048), (32768, 65536, 4096))
+
+UNIT_BINS = 4096
+UNITS = 65536 // UNIT_BINS
+PART_PASSES = UNIT_BINS // K_PASS
+BANK_PASSES = 4
+PIECE_PASSES = 2
+UNIT_PIECES = 2 * PART_PASSES // PIECE_PASSES
+PIECE_COUNT = 256
+DOUBLE_PASSES = 2 * PART_PASSES
+UNIT_BANKS = 2 * PART_PASSES // BANK_PASSES
+TILE_PASSES = 2
+UNIT_TILES = 2 * PART_PASSES // TILE_PASSES
+
+MEAN_BEHIND_TILE = 0
+VAR_BEHIND_TILE = 1
+SCALE_BEHIND_TILE = 3
+W_RUN_PASSES = 4
+
+FLOPS = 2 * 131072 * T * N_OUT
+
+
+def group_of_unit(u):
+    for gi, (first_bin, end_bin, band_bins) in enumerate(GROUP_BINS):
+        if first_bin <= u * UNIT_BINS < end_bin:
+            return gi
+    raise ValueError("no such unit")
+
+
+def half_passes_of_unit(u):
+    return GROUP_BINS[group_of_unit(u)][2] // K_PASS
+
+
+def tile_bandsplitmodule_k_kernel(
+    tc, x_real, x_imag, sample_rate,
+    g16, b16, W16, c16, g32, b32, W32, c32, g64, b64, W64, c64, out,
+):
+    nc = tc.nc
+    weights = (W16, W32, W64)
+
+    with ExitStack() as stack:
+        const = stack.enter_context(tc.tile_pool(name="const", bufs=1))
+        setup = stack.enter_context(tc.tile_pool(name="setup", bufs=1))
+        xk_pool = stack.enter_context(tc.tile_pool(name="xk", bufs=6))
+        xh_pool = stack.enter_context(tc.tile_pool(name="xh", bufs=6))
+        y_pool = stack.enter_context(tc.tile_pool(name="y", bufs=3))
+        gx_pool = stack.enter_context(tc.tile_pool(name="gx", bufs=3))
+        xq_pool = stack.enter_context(tc.tile_pool(name="xq", bufs=2))
+        wk_pool = stack.enter_context(tc.tile_pool(name="wk", bufs=2))
+        gw_pool = stack.enter_context(tc.tile_pool(name="gw", bufs=2))
+        wq_pool = stack.enter_context(tc.tile_pool(name="wq", bufs=2))
+        small = stack.enter_context(tc.tile_pool(name="small", bufs=3))
+        ring = stack.enter_context(tc.psum_pool(name="ring", bufs=4))
+        back = stack.enter_context(tc.psum_pool(name="back", bufs=2))
+        fold_ps = stack.enter_context(tc.psum_pool(name="fold_ps", bufs=1))
+        acc_ps = stack.enter_context(tc.psum_pool(name="acc_ps", bufs=1))
+        stack.enter_context(tc.manual_schedule())
+
+        def load_x(u):
+            tiles = []
+            for x_part in (x_real, x_imag):
+                xk = xk_pool.tile([P, PART_PASSES, PACK * T], BF16)
+                rows = x_part[0, u * UNIT_BINS : (u + 1) * UNIT_BINS, :]
+                nc.sync.dma_start(out=xk[:], in_=rows.rearrange("(s p j) t -> p s (j t)", p=P, j=PACK))
+                tiles.append(xk)
+            return tiles
+
+        def load_w(d):
+            gi = group_of_unit(2 * d)
+            first_double = GROUP_BINS[gi][0] // (2 * UNIT_BINS)
+            rows = weights[gi].rearrange("k c n -> (k c) n")
+            wk = wk_pool.tile([P, 2 * DOUBLE_PASSES, PACK * N_OUT], BF16)
+            for a in range(4):
+                first = ((d - first_double) * 4 + a) * PART_PASSES * K_PASS
+                nc.sync.dma_start(
+                    out=wk[:, a * PART_PASSES : (a + 1) * PART_PASSES, :],
+                    in_=rows[first : first + PART_PASSES * K_PASS, :].rearrange(
+                        "(s p j) n -> p s (j n)", p=P, j=PACK
+                    ),
+                )
+            return wk
+
+        x_tiles = {0: load_x(0)}
+        w_tiles = {0: load_w(0)}
+        x_tiles[1] = load_x(1)
+
+        one = const.tile([P, 1], F32)
+        nc.vector.memset(one[:], 1.0)
+        warm = const.tile([P, 1], F32)
+        nc.scalar.activation(out=warm[:], in_=one[:], func=ACT.Sqrt)
+
+        ident = const.tile([P, P], F32)
+        make_identity(nc, ident[:])
+
+        eye32 = setup.tile([P, 32], F32)
+        nc.vector.tensor_reduce(
+            out=eye32[:], in_=ident[:].rearrange("p (b m) -> p m b", b=4), axis=AX.X, op=ALU.add
+        )
+        folds = []
+        for gi, (first_bin, end_bin, band_bins) in enumerate(GROUP_BINS):
+            results = 2 * band_bins // PIECE_COUNT
+            fold = const.tile([P, 4, 32], F32, name="fold%d" % gi)
+            nc.vector.tensor_scalar(
+                out=fold[:], in0=eye32[:].unsqueeze(1).to_broadcast([P, 4, 32]),
+                scalar1=1.0 / results, scalar2=None, op0=ALU.mult,
+            )
+            folds.append(fold)
+
+        def load_channel_vector(v16, v32, v64, name):
+            nat = setup.tile([P, 2 * K_PASS], BF16, name=name + "_nat")
+            nc.scalar.dma_start(out=nat[0:32, :], in_=v16.rearrange("k (a c) -> (k a) c", c=2 * K_PASS))
+            nc.scalar.dma_start(out=nat[32:64, :], in_=v32.rearrange("k (a c) -> (k a) c", c=2 * K_PASS))
+            nc.scalar.dma_start(out=nat[64:128, :], in_=v64.rearrange("k (a c) -> (k a) c", c=2 * K_PASS))
+            perm = setup.tile([P, 2, PACK, P], F32, name=name + "_perm")
+            nc.vector.tensor_copy(out=perm[:], in_=nat[:].rearrange("q (c p j) -> q c j p", c=2, j=PACK))
+            return perm
+
+        def turn_channel_vector(perm, c):
+            turned = back.tile([P, PACK, P], F32, tag="xb", name="turned")
+            for j in range(PACK):
+                nc.tensor.transpose(out=turned[:, j, :], in_=perm[:, c, j, :], identity=ident[:])
+            return turned
+
+        gain_perm = load_channel_vector(g16, g32, g64, "gain")
+        shift_perm = load_channel_vector(b16, b32, b64, "shift")
+        gain_cols = const.tile([P, P, 2, PACK], F32)
+        shift_cols = const.tile([P, P, 2, PACK], F32)
+        gain = gain_cols[:].rearrange("p q c j -> p (q c j)")
+        shift = shift_cols[:].rearrange("p q c j -> p (q c j)")
+
+        c_nat = setup.tile([P, P], BF16)
+        nc.vector.memset(c_nat[:], 0.0)
+        nc.scalar.dma_start(out=c_nat[0:8, :], in_=c16.rearrange("(g a) n -> g (a n)", a=2))
+        nc.scalar.dma_start(out=c_nat[8:12, :], in_=c32.rearrange("(g a) n -> g (a n)", a=2))
+        nc.scalar.dma_start(out=c_nat[12:16, :], in_=c64.rearrange("(g a) n -> g (a n)", a=2))
+        c_f32 = setup.tile([P, P], F32)
+        nc.vector.tensor_copy(out=c_f32[:], in_=c_nat[:])
+        bias = const.tile([P, P], F32)
+
+        result = const.tile([P, 16, 2 * T], F32)
+
+        banks = [(part, kb) for part in range(2) for kb in range(PART_PASSES // BANK_PASSES)]
+        xts = {}
+        xhs = {}
+        ys = {}
+        st = {}
+        xqs = {}
+        wqs = {}
+
+        def transpose_and_count(u, n):
+            part, kb = banks[n]
+            half = half_passes_of_unit(u)
+            xk = x_tiles[u][part]
+            if n == 0:
+                stats = small.tile([P, UNIT_PIECES, 6], F32)
+                st[u, "stats"] = stats
+            xt = ring.tile([P, BANK_PASSES * P], F32)
+            for a in range(BANK_PASSES):
+                nc.tensor.transpose(
+                    out=xt[:, a * P : (a + 1) * P],
+                    in_=xk[:, kb * BANK_PASSES + a, :].bitcast(F32),
+                    identity=ident[:],
+                )
+            for h in range(BANK_PASSES // PIECE_PASSES):
+                i = kb * BANK_PASSES + h * PIECE_PASSES
+                pieces_per_half = half // PIECE_PASSES
+                piece = (i // half) * 2 * pieces_per_half + part * pieces_per_half + (i % half) // PIECE_PASSES
+                nc.vector.bn_stats(
+                    out=st[u, "stats"][:, piece, :],
+                    in_=xt[:, h * PIECE_PASSES * P : (h + 1) * PIECE_PASSES * P].bitcast(BF16),
+                )
+            xts[u, n] = xt
+
+        def stats_mean(u, fill):
+            gi = group_of_unit(u)
+            bands = UNIT_BINS // GROUP_BINS[gi][2]
+            fields = st[u, "stats"][:].rearrange("p k (e f) -> p k e f", f=3)
+            means = fields[:, :, :, 1]
+            squares = fields[:, :, :, 2]
+            mean_ps = fold_ps.tile([P, 2 * UNIT_PIECES], F32, tag="fold")
+            nc.tensor.matmul(
+                out=mean_ps[:], lhsT=folds[gi][:].rearrange("p b m -> p (b m)"),
+                rhs=means.rearrange("p k e -> p (k e)"), start=True, stop=True,
+            )
+            inner = small.tile([P, UNIT_PIECES, 2], F32)
+            nc.vector.tensor_scalar(
+                out=inner[:], in0=squares, scalar1=1.0 / PIECE_COUNT, scalar2=EPS, op0=ALU.mult, op1=ALU.add
+            )
+            fill()
+            neg_mean = small.tile([P, bands, 2], F32)
+            nc.vector.tensor_reduce(
+                out=neg_mean[:], in_=mean_ps[:].rearrange("p (b k e) -> p b e k", b=bands, e=2),
+                axis=AX.X, op=ALU.add, negate=True,
+            )
+            dev = small.tile([P, UNIT_PIECES, 2], F32)
+            nc.vector.tensor_tensor(
+                out=dev[:].rearrange("p (b k) e -> p b k e", b=bands),
+                in0=means.rearrange("p (b k) e -> p b k e", b=bands),
+                in1=neg_mean[:].unsqueeze(2).to_broadcast([P, bands, UNIT_PIECES // bands, 2]),
+                op=ALU.add,
+            )
+            dev_sq = small.tile([P, UNIT_PIECES, 2], F32)
+            nc.vector.tensor_tensor(out=dev_sq[:], in0=dev[:], in1=dev[:], op=ALU.mult)
+            spread = small.tile([P, UNIT_PIECES, 2], F32)
+            nc.vector.tensor_tensor(out=spread[:], in0=dev_sq[:], in1=inner[:], op=ALU.add)
+            st[u, "neg_mean"] = neg_mean
+            st[u, "spread"] = spread
+
+        def stats_var(u, fill):
+            gi = group_of_unit(u)
+            bands = UNIT_BINS // GROUP_BINS[gi][2]
+            var_ps = fold_ps.tile([P, 2 * UNIT_PIECES], F32, tag="fold")
+            nc.tensor.matmul(
+                out=var_ps[:], lhsT=folds[gi][:].rearrange("p b m -> p (b m)"),
+                rhs=st[u, "spread"][:].rearrange("p k e -> p (k e)"), start=True, stop=True,
+            )
+            fill()
+            var = small.tile([P, bands, 2], F32)
+            nc.vector.tensor_reduce(
+                out=var[:], in_=var_ps[:].rearrange("p (b k e) -> p b e k", b=bands, e=2),
+                axis=AX.X, op=ALU.add,
+            )
+            st[u, "var"] = var
+
+        def stats_scale(u, fill):
+            bands = UNIT_BINS // GROUP_BINS[group_of_unit(u)][2]
+            std = small.tile([P, bands, 2], F32)
+            nc.scalar.activation(out=std[:], in_=st[u, "var"][:], func=ACT.Sqrt)
+            fill()
+            rstd = small.tile([P, bands, 2], F32)
+            nc.vector.reciprocal(out=rstd[:], in_=std[:])
+            offset = small.tile([P, bands, 2], F32)
+            nc.vector.tensor_tensor(out=offset[:], in0=st[u, "neg_mean"][:], in1=rstd[:], op=ALU.mult)
+            st[u, "rstd"] = rstd
+            st[u, "offset"] = offset
+
+        def normalise(u, n):
+            part, kb = banks[n]
+            half = half_passes_of_unit(u)
+            run = min(half, BANK_PASSES)
+            xh = xh_pool.tile([P, 2, BANK_PASSES, P], F32)
+            halves = xts[u, n][:].bitcast(BF16).rearrange("p (s w e) -> p s w e", s=BANK_PASSES, e=2)
+            for s0 in range(0, BANK_PASSES, run):
+                band = (kb * BANK_PASSES + s0) // half
+                for e in range(2):
+                    nc.scalar.activation(
+                        out=xh[:, e, s0 : s0 + run, :], in_=halves[:, s0 : s0 + run, :, e], func=ACT.Identity,
+                        bias=st[u, "offset"][:, band, e : e + 1], scale=st[u, "rstd"][:, band, e : e + 1],
+                    )
+            xhs[u, n] = xh
+
+        xbs = {}
+
+        def back_transpose(u, m):
+            xh = xhs[u, m * TILE_PASSES // BANK_PASSES]
+            xb = back.tile([P, TILE_PASSES, 2, P], F32)
+            for a in range(TILE_PASSES):
+                for e in range(2):
+                    nc.tensor.transpose(
+                        out=xb[:, a, e, :], in_=xh[:, e, (m * TILE_PASSES + a) % BANK_PASSES, :], identity=ident[:]
+                    )
+            xbs[u, m] = xb
+
+        def gain_and_shift(u, m):
+            half = half_passes_of_unit(u)
+            part = m * TILE_PASSES // PART_PASSES
+            if m * TILE_PASSES % PART_PASSES == 0:
+                y = y_pool.tile([P, PACK, PART_PASSES, T], BF16)
+                ys[u, part] = y
+            for a in range(TILE_PASSES):
+                i = (m * TILE_PASSES + a) % PART_PASSES
+                row_pass = 2 * PART_PASSES * u + (i // half) * 2 * half + part * half + i % half
+                for j in range(PACK):
+                    col = row_pass * PACK + j
+                    nc.scalar.activation(
+                        out=ys[u, part][:, j, i, :].rearrange("p (e w) -> p e w", e=2),
+                        in_=xbs[u, m][:, a, :, 32 * j : 32 * (j + 1)], func=ACT.Identity,
+                        bias=shift[:, col : col + 1], scale=gain[:, col : col + 1],
+                    )
+
+        def quantise_x(u, part):
+            half = half_passes_of_unit(u)
+            bands = PART_PASSES // half
+            if u % 2 == 0 and part == 0:
+                xq = xq_pool.tile([P, DOUBLE_PASSES, 2 * T], U32, align_bytes=64)
+                xs = xq_pool.tile([P, DOUBLE_PASSES, 2 * T], U8, align_bytes=64)
+                xqs[u // 2] = (xq, xs)
+            xq, xs = xqs[u // 2]
+            gx = gx_pool.tile([P, PART_PASSES, PACK * T], BF16, align_bytes=64)
+            nc.vector.tensor_copy(
+                out=gx[:].rearrange("p s (m i j) -> p (s m) j i", i=4, j=PACK),
+                in_=ys[u, part][:].rearrange("p j s (m i) -> p (s m) j i", i=4),
+            )
+            for i in range(PART_PASSES):
+                band_in_double = (u % 2) * bands + i // half
+                pair, side = divmod(band_in_double, 2)
+                slot = pair * 2 * half + part * half + i % half
+                nc.vector.quantize_mx(
+                    out=xq[:, slot, side * T : (side + 1) * T].bitcast(FP8X4),
+                    scales=xs[:, slot, side * T : (side + 1) * T],
+                    in_=gx[:, i, :],
+                )
+
+        gws = {}
+
+        def regroup_w_runs(u):
+            half = half_passes_of_unit(u)
+            run = W_RUN_PASSES
+            first_slot = (u % 2) * PART_PASSES
+            runs = []
+            for slot in range(first_slot, first_slot + PART_PASSES, run):
+                for side in range(2):
+                    runs.append((slot // (2 * half) * 2 + side, slot % (2 * half), run))
+            return runs
+
+        def regroup_w(u, band_in_double, first_pass, run):
+            half = half_passes_of_unit(u)
+            pair, side = divmod(band_in_double, 2)
+            slot = pair * 2 * half + first_pass - (u % 2) * PART_PASSES
+            raw = band_in_double * 2 * half + first_pass
+            nc.vector.tensor_copy(
+                out=gws[u][:, slot : slot + run, side, :].rearrange("p c (m i j) -> p c m j i", i=4, j=PACK),
+                in_=w_tiles[u // 2][:, raw : raw + run, :].rearrange("p c (j m i) -> p c m j i", j=PACK, i=4),
+            )
+
+        def quantise_w(u):
+            if u % 2 == 0:
+                wq = wq_pool.tile([P, DOUBLE_PASSES, 2 * N_OUT], U32, align_bytes=64)
+                ws = wq_pool.tile([P, DOUBLE_PASSES, 2 * N_OUT], U8, align_bytes=64)
+                wqs[u // 2] = (wq, ws)
+            wq, ws = wqs[u // 2]
+            slots = slice((u % 2) * PART_PASSES, (u % 2 + 1) * PART_PASSES)
+            nc.vector.quantize_mx(
+                out=wq[:, slots, :].rearrange("p c m -> p (c m)").bitcast(FP8X4),
+                scales=ws[:, slots, :].rearrange("p c m -> p (c m)"),
+                in_=gws[u][:].rearrange("p c a m -> p (c a m)"),
+            )
+
+        def multiply_and_store(d):
+            half = half_passes_of_unit(2 * d)
+            pairs = DOUBLE_PASSES // (2 * half)
+            first_pair = sum(PART_PASSES // half_passes_of_unit(2 * dd) for dd in range(d))
+            wq, ws = wqs[d]
+            xq, xs = xqs[d]
+            acc = acc_ps.tile([P, pairs, 2 * T], F32)
+            for pair in range(pairs):
+                for c in range(2 * half):
+                    slot = pair * 2 * half + c
+                    nc.tensor.matmul_mx(
+                        out=acc[:, pair, :],
+                        lhsT=wq[:, slot, :].bitcast(FP8X4), lhsT_scale=ws[:, slot, :],
+                        rhs=xq[:, slot, :].bitcast(FP8X4), rhs_scale=xs[:, slot, :],
+                        start=(c == 0), stop=(c == 2 * half - 1),
+                    )
+            for pair in range(pairs):
+                nc.vector.tensor_scalar(
+                    out=result[:, first_pair + pair, :].rearrange("p (a w e) -> p a w e", a=2, e=2),
+                    in0=acc[:, pair, :].rearrange("p (a e w) -> p a w e", a=2, e=2),
+                    scalar1=bias[:, first_pair + pair : first_pair + pair + 1], scalar2=None, op0=ALU.add,
+                )
+            by_side = out[0].rearrange("n (g a) t -> a n g t", a=2)
+            for side in range(2):
+                nc.sync.dma_start(
+                    out=by_side[side, :, first_pair : first_pair + pairs, :],
+                    in_=result[side * N_OUT : (side + 1) * N_OUT, first_pair : first_pair + pairs, side * T : (side + 1) * T],
+                )
+
+        for n in range(UNIT_BANKS):
+            transpose_and_count(0, n)
+        gain_turned = [turn_channel_vector(gain_perm, c) for c in range(2)]
+        def nothing():
+            return None
+
+        stats_mean(0, nothing)
+        for c in range(2):
+            nc.vector.tensor_copy(out=gain_cols[:, :, c, :], in_=gain_turned[c][:].rearrange("p j q -> p q j"))
+        shift_turned = [turn_channel_vector(shift_perm, c) for c in range(2)]
+        stats_var(0, nothing)
+        for c in range(2):
+            nc.vector.tensor_copy(out=shift_cols[:, :, c, :], in_=shift_turned[c][:].rearrange("p j q -> p q j"))
+        c_turned = back.tile([P, P], F32, tag="xb")
+        nc.tensor.transpose(out=c_turned[:], in_=c_f32[:], identity=ident[:])
+        stats_scale(0, nothing)
+        nc.vector.tensor_copy(out=bias[:], in_=c_turned[:])
+
+        for u in range(UNITS):
+            more = u + 1 < UNITS
+            if u + 2 < UNITS:
+                x_tiles[u + 2] = load_x(u + 2)
+            if u % 2 == 0 and u // 2 + 1 < UNITS // 2:
+                w_tiles[u // 2 + 1] = load_w(u // 2 + 1)
+            if u >= 1:
+                quantise_x(u - 1, 1)
+            if u >= 3 and u % 2 == 1:
+                multiply_and_store((u - 3) // 2)
+
+            for n in range(UNIT_BANKS):
+                normalise(u, n)
+                if more:
+                    transpose_and_count(u + 1, n)
+                if n == 0:
+                    back_transpose(u, 0)
+                    back_transpose(u, 1)
+
+            gw = gw_pool.tile([P, PART_PASSES, 2, PACK * N_OUT], BF16, align_bytes=64)
+            gws[u] = gw
+            runs = regroup_w_runs(u)
+
+            def regroup_first():
+                regroup_w(u, *runs[0])
+
+            def regroup_second():
+                regroup_w(u, *runs[1])
+
+            def regroup_rest():
+                regroup_w(u, *runs[2])
+                regroup_w(u, *runs[3])
+
+            for m in range(UNIT_TILES):
+                gain_and_shift(u, m)
+                if m + 2 < UNIT_TILES:
+                    back_transpose(u, m + 2)
+                if more and m == MEAN_BEHIND_TILE:
+                    stats_mean(u + 1, regroup_first)
+                if more and m == VAR_BEHIND_TILE:
+                    stats_var(u + 1, regroup_second)
+                if more and m == SCALE_BEHIND_TILE:
+                    stats_scale(u + 1, regroup_rest)
+                    quantise_w(u)
+                    quantise_x(u, 0)
+            if not more:
+                regroup_first()
+                regroup_second()
+                regroup_rest()
+                quantise_w(u)
+                quantise_x(u, 0)
+
+        quantise_x(UNITS - 1, 1)
+        multiply_and_store(UNITS // 2 - 1)

@@ -32,6 +32,7 @@ DOUBLE_PASSES = 2 * PART_PASSES
 UNIT_BANKS = 2 * PART_PASSES // BANK_PASSES
 TILE_PASSES = 2
 UNIT_TILES = 2 * PART_PASSES // TILE_PASSES
+BACK_BANKS = 3
 
 MEAN_BEHIND_TILE = 0
 VAR_BEHIND_TILE = 1
@@ -72,9 +73,8 @@ def tile_bandsplitmodule_k_kernel(
         wq_pool = stack.enter_context(tc.tile_pool(name="wq", bufs=2))
         small = stack.enter_context(tc.tile_pool(name="small", bufs=3))
         ring = stack.enter_context(tc.psum_pool(name="ring", bufs=4))
-        back = stack.enter_context(tc.psum_pool(name="back", bufs=2))
+        back = stack.enter_context(tc.psum_pool(name="back", bufs=BACK_BANKS))
         fold_ps = stack.enter_context(tc.psum_pool(name="fold_ps", bufs=1))
-        acc_ps = stack.enter_context(tc.psum_pool(name="acc_ps", bufs=1))
         stack.enter_context(tc.manual_schedule())
 
         def load_x(u):
@@ -101,14 +101,8 @@ def tile_bandsplitmodule_k_kernel(
                 )
             return wk
 
-        x_tiles = {0: load_x(0)}
+        x_tiles = {0: load_x(0), 1: load_x(1)}
         w_tiles = {0: load_w(0)}
-        x_tiles[1] = load_x(1)
-
-        one = const.tile([P, 1], F32)
-        nc.vector.memset(one[:], 1.0)
-        warm = const.tile([P, 1], F32)
-        nc.scalar.activation(out=warm[:], in_=one[:], func=ACT.Sqrt)
 
         ident = const.tile([P, P], F32)
         make_identity(nc, ident[:])
@@ -132,6 +126,9 @@ def tile_bandsplitmodule_k_kernel(
             nc.scalar.dma_start(out=nat[0:32, :], in_=v16.rearrange("k (a c) -> (k a) c", c=2 * K_PASS))
             nc.scalar.dma_start(out=nat[32:64, :], in_=v32.rearrange("k (a c) -> (k a) c", c=2 * K_PASS))
             nc.scalar.dma_start(out=nat[64:128, :], in_=v64.rearrange("k (a c) -> (k a) c", c=2 * K_PASS))
+            return nat
+
+        def sort_channel_vector(nat, name):
             perm = setup.tile([P, 2, PACK, P], F32, name=name + "_perm")
             nc.vector.tensor_copy(out=perm[:], in_=nat[:].rearrange("q (c p j) -> q c j p", c=2, j=PACK))
             return perm
@@ -142,8 +139,8 @@ def tile_bandsplitmodule_k_kernel(
                 nc.tensor.transpose(out=turned[:, j, :], in_=perm[:, c, j, :], identity=ident[:])
             return turned
 
-        gain_perm = load_channel_vector(g16, g32, g64, "gain")
-        shift_perm = load_channel_vector(b16, b32, b64, "shift")
+        gain_nat = load_channel_vector(g16, g32, g64, "gain")
+        shift_nat = load_channel_vector(b16, b32, b64, "shift")
         gain_cols = const.tile([P, P, 2, PACK], F32)
         shift_cols = const.tile([P, P, 2, PACK], F32)
         gain = gain_cols[:].rearrange("p q c j -> p (q c j)")
@@ -154,9 +151,12 @@ def tile_bandsplitmodule_k_kernel(
         nc.scalar.dma_start(out=c_nat[0:8, :], in_=c16.rearrange("(g a) n -> g (a n)", a=2))
         nc.scalar.dma_start(out=c_nat[8:12, :], in_=c32.rearrange("(g a) n -> g (a n)", a=2))
         nc.scalar.dma_start(out=c_nat[12:16, :], in_=c64.rearrange("(g a) n -> g (a n)", a=2))
-        c_f32 = setup.tile([P, P], F32)
-        nc.vector.tensor_copy(out=c_f32[:], in_=c_nat[:])
         bias = const.tile([P, P], F32)
+
+        one = const.tile([P, 1], F32)
+        nc.vector.memset(one[:], 1.0)
+        warm = const.tile([P, 1], F32)
+        nc.scalar.activation(out=warm[:], in_=one[:], func=ACT.Sqrt)
 
         result = const.tile([P, 16, 2 * T], F32)
 
@@ -363,7 +363,7 @@ def tile_bandsplitmodule_k_kernel(
             first_pair = sum(PART_PASSES // half_passes_of_unit(2 * dd) for dd in range(d))
             wq, ws = wqs[d]
             xq, xs = xqs[d]
-            acc = acc_ps.tile([P, pairs, 2 * T], F32)
+            acc = back.tile([P, pairs, 2 * T], F32, tag="xb")
             for pair in range(pairs):
                 for c in range(2 * half):
                     slot = pair * 2 * half + c
@@ -386,22 +386,24 @@ def tile_bandsplitmodule_k_kernel(
                     in_=result[side * N_OUT : (side + 1) * N_OUT, first_pair : first_pair + pairs, side * T : (side + 1) * T],
                 )
 
-        for n in range(UNIT_BANKS):
-            transpose_and_count(0, n)
-        gain_turned = [turn_channel_vector(gain_perm, c) for c in range(2)]
         def nothing():
             return None
 
+        for n in range(UNIT_BANKS):
+            transpose_and_count(0, n)
         stats_mean(0, nothing)
-        for c in range(2):
-            nc.vector.tensor_copy(out=gain_cols[:, :, c, :], in_=gain_turned[c][:].rearrange("p j q -> p q j"))
-        shift_turned = [turn_channel_vector(shift_perm, c) for c in range(2)]
+        gain_perm = sort_channel_vector(gain_nat, "gain")
         stats_var(0, nothing)
-        for c in range(2):
-            nc.vector.tensor_copy(out=shift_cols[:, :, c, :], in_=shift_turned[c][:].rearrange("p j q -> p q j"))
+        shift_perm = sort_channel_vector(shift_nat, "shift")
+        stats_scale(0, nothing)
+        for perm, cols in ((gain_perm, gain_cols), (shift_perm, shift_cols)):
+            for c in range(2):
+                turned = turn_channel_vector(perm, c)
+                nc.vector.tensor_copy(out=cols[:, :, c, :], in_=turned[:].rearrange("p j q -> p q j"))
+        c_f32 = setup.tile([P, P], F32)
+        nc.vector.tensor_copy(out=c_f32[:], in_=c_nat[:])
         c_turned = back.tile([P, P], F32, tag="xb")
         nc.tensor.transpose(out=c_turned[:], in_=c_f32[:], identity=ident[:])
-        stats_scale(0, nothing)
         nc.vector.tensor_copy(out=bias[:], in_=c_turned[:])
 
         for u in range(UNITS):
@@ -419,9 +421,9 @@ def tile_bandsplitmodule_k_kernel(
                 normalise(u, n)
                 if more:
                     transpose_and_count(u + 1, n)
-                if n == 0:
-                    back_transpose(u, 0)
-                    back_transpose(u, 1)
+                for m in range(BACK_BANKS):
+                    if m * TILE_PASSES // BANK_PASSES == n:
+                        back_transpose(u, m)
 
             gw = gw_pool.tile([P, PART_PASSES, 2, PACK * N_OUT], BF16, align_bytes=64)
             gws[u] = gw
@@ -439,8 +441,8 @@ def tile_bandsplitmodule_k_kernel(
 
             for m in range(UNIT_TILES):
                 gain_and_shift(u, m)
-                if m + 2 < UNIT_TILES:
-                    back_transpose(u, m + 2)
+                if m + BACK_BANKS < UNIT_TILES:
+                    back_transpose(u, m + BACK_BANKS)
                 if more and m == MEAN_BEHIND_TILE:
                     stats_mean(u + 1, regroup_first)
                 if more and m == VAR_BEHIND_TILE:

@@ -34,10 +34,12 @@ TILE_PASSES = 2
 UNIT_TILES = 2 * PART_PASSES // TILE_PASSES
 BACK_BANKS = 3
 
-MEAN_BEHIND_TILE = 0
-VAR_BEHIND_TILE = 1
-SCALE_BEHIND_TILE = 3
+MEAN_BEHIND_TILE = 2
+VAR_BEHIND_TILE = 4
+SCALE_BEHIND_TILE = 6
+VECTOR_TILES = 1
 W_RUN_PASSES = 4
+GPSIMD_W_RUNS = 3
 
 FLOPS = 2 * 131072 * T * N_OUT
 
@@ -69,7 +71,7 @@ def tile_bandsplitmodule_k_kernel(
         gx_pool = stack.enter_context(tc.tile_pool(name="gx", bufs=3))
         xq_pool = stack.enter_context(tc.tile_pool(name="xq", bufs=2))
         wk_pool = stack.enter_context(tc.tile_pool(name="wk", bufs=2))
-        gw_pool = stack.enter_context(tc.tile_pool(name="gw", bufs=2))
+        gw_pool = stack.enter_context(tc.tile_pool(name="gw", bufs=1))
         wq_pool = stack.enter_context(tc.tile_pool(name="wq", bufs=2))
         small = stack.enter_context(tc.tile_pool(name="small", bufs=3))
         ring = stack.enter_context(tc.psum_pool(name="ring", bufs=4))
@@ -293,13 +295,30 @@ def tile_bandsplitmodule_k_kernel(
                 row_pass = 2 * PART_PASSES * u + (i // half) * 2 * half + part * half + i % half
                 for j in range(PACK):
                     col = row_pass * PACK + j
-                    nc.scalar.activation(
-                        out=ys[u, part][:, j, i, :].rearrange("p (e w) -> p e w", e=2),
-                        in_=xbs[u, m][:, a, :, 32 * j : 32 * (j + 1)], func=ACT.Identity,
-                        bias=shift[:, col : col + 1], scale=gain[:, col : col + 1],
-                    )
+                    dst = ys[u, part][:, j, i, :].rearrange("p (e w) -> p e w", e=2)
+                    src = xbs[u, m][:, a, :, 32 * j : 32 * (j + 1)]
+                    if m < VECTOR_TILES:
+                        nc.vector.tensor_scalar(
+                            out=dst, in0=src, scalar1=gain[:, col : col + 1], scalar2=shift[:, col : col + 1],
+                            op0=ALU.mult, op1=ALU.add,
+                        )
+                    else:
+                        nc.scalar.activation(
+                            out=dst, in_=src, func=ACT.Identity,
+                            bias=shift[:, col : col + 1], scale=gain[:, col : col + 1],
+                        )
 
-        def quantise_x(u, part):
+        gxs = {}
+
+        def regroup_x_part(u, part):
+            gx = gx_pool.tile([P, PART_PASSES, PACK * T], BF16, align_bytes=64)
+            nc.vector.tensor_copy(
+                out=gx[:].rearrange("p s (m i j) -> p (s m) j i", i=4, j=PACK),
+                in_=ys[u, part][:].rearrange("p j s (m i) -> p (s m) j i", i=4),
+            )
+            gxs[u, part] = gx
+
+        def quantise_x_part(u, part):
             half = half_passes_of_unit(u)
             bands = PART_PASSES // half
             if u % 2 == 0 and part == 0:
@@ -307,11 +326,7 @@ def tile_bandsplitmodule_k_kernel(
                 xs = xq_pool.tile([P, DOUBLE_PASSES, 2 * T], U8, align_bytes=64)
                 xqs[u // 2] = (xq, xs)
             xq, xs = xqs[u // 2]
-            gx = gx_pool.tile([P, PART_PASSES, PACK * T], BF16, align_bytes=64)
-            nc.vector.tensor_copy(
-                out=gx[:].rearrange("p s (m i j) -> p (s m) j i", i=4, j=PACK),
-                in_=ys[u, part][:].rearrange("p j s (m i) -> p (s m) j i", i=4),
-            )
+            gx = gxs[u, part]
             for i in range(PART_PASSES):
                 band_in_double = (u % 2) * bands + i // half
                 pair, side = divmod(band_in_double, 2)
@@ -321,6 +336,10 @@ def tile_bandsplitmodule_k_kernel(
                     scales=xs[:, slot, side * T : (side + 1) * T],
                     in_=gx[:, i, :],
                 )
+
+        def quantise_x(u, part):
+            regroup_x_part(u, part)
+            quantise_x_part(u, part)
 
         gws = {}
 
@@ -334,15 +353,24 @@ def tile_bandsplitmodule_k_kernel(
                     runs.append((slot // (2 * half) * 2 + side, slot % (2 * half), run))
             return runs
 
-        def regroup_w(u, band_in_double, first_pass, run):
+        def regroup_w(u, on_gpsimd, band_in_double, first_pass, run):
             half = half_passes_of_unit(u)
             pair, side = divmod(band_in_double, 2)
             slot = pair * 2 * half + first_pass - (u % 2) * PART_PASSES
             raw = band_in_double * 2 * half + first_pass
-            nc.vector.tensor_copy(
-                out=gws[u][:, slot : slot + run, side, :].rearrange("p c (m i j) -> p c m j i", i=4, j=PACK),
-                in_=w_tiles[u // 2][:, raw : raw + run, :].rearrange("p c (j m i) -> p c m j i", j=PACK, i=4),
-            )
+            grouped = gws[u][:, slot : slot + run, side, :]
+            rows = w_tiles[u // 2][:, raw : raw + run, :]
+            if on_gpsimd:
+                nc.gpsimd.tensor_scalar(
+                    out=grouped.rearrange("p c (n j) -> p c n j", j=PACK),
+                    in0=rows.rearrange("p c (j n) -> p c n j", j=PACK),
+                    scalar1=1.0, scalar2=0.0, op0=ALU.mult, op1=ALU.add,
+                )
+            else:
+                nc.vector.tensor_copy(
+                    out=grouped.rearrange("p c (m i j) -> p c m j i", i=4, j=PACK),
+                    in_=rows.rearrange("p c (j m i) -> p c m j i", j=PACK, i=4),
+                )
 
         def quantise_w(u):
             if u % 2 == 0:
@@ -414,8 +442,15 @@ def tile_bandsplitmodule_k_kernel(
                 w_tiles[u // 2 + 1] = load_w(u // 2 + 1)
             if u >= 1:
                 quantise_x(u - 1, 1)
+                quantise_w(u - 1)
             if u >= 3 and u % 2 == 1:
                 multiply_and_store((u - 3) // 2)
+
+            gw = gw_pool.tile([P, PART_PASSES, 2, PACK * N_OUT], BF16, align_bytes=64)
+            gws[u] = gw
+            runs = regroup_w_runs(u)
+            for r in range(GPSIMD_W_RUNS):
+                regroup_w(u, True, *runs[r])
 
             for n in range(UNIT_BANKS):
                 normalise(u, n)
@@ -424,39 +459,36 @@ def tile_bandsplitmodule_k_kernel(
                 for m in range(BACK_BANKS):
                     if m * TILE_PASSES // BANK_PASSES == n:
                         back_transpose(u, m)
-
-            gw = gw_pool.tile([P, PART_PASSES, 2, PACK * N_OUT], BF16, align_bytes=64)
-            gws[u] = gw
-            runs = regroup_w_runs(u)
-
-            def regroup_first():
-                regroup_w(u, *runs[0])
-
-            def regroup_second():
-                regroup_w(u, *runs[1])
+                        if m < VECTOR_TILES:
+                            gain_and_shift(u, m)
+            for m in range(VECTOR_TILES):
+                back_transpose(u, m + BACK_BANKS)
 
             def regroup_rest():
-                regroup_w(u, *runs[2])
-                regroup_w(u, *runs[3])
+                for r in range(GPSIMD_W_RUNS, len(runs)):
+                    regroup_w(u, False, *runs[r])
 
-            for m in range(UNIT_TILES):
+            def regroup_x():
+                regroup_x_part(u, 0)
+
+            def quantise_x_real():
+                quantise_x_part(u, 0)
+
+            for m in range(VECTOR_TILES, UNIT_TILES):
                 gain_and_shift(u, m)
                 if m + BACK_BANKS < UNIT_TILES:
                     back_transpose(u, m + BACK_BANKS)
                 if more and m == MEAN_BEHIND_TILE:
-                    stats_mean(u + 1, regroup_first)
+                    stats_mean(u + 1, regroup_rest)
                 if more and m == VAR_BEHIND_TILE:
-                    stats_var(u + 1, regroup_second)
+                    stats_var(u + 1, regroup_x)
                 if more and m == SCALE_BEHIND_TILE:
-                    stats_scale(u + 1, regroup_rest)
-                    quantise_w(u)
-                    quantise_x(u, 0)
+                    stats_scale(u + 1, quantise_x_real)
             if not more:
-                regroup_first()
-                regroup_second()
                 regroup_rest()
-                quantise_w(u)
-                quantise_x(u, 0)
+                regroup_x()
+                quantise_x_real()
 
         quantise_x(UNITS - 1, 1)
+        quantise_w(UNITS - 1)
         multiply_and_store(UNITS // 2 - 1)

@@ -37,7 +37,7 @@ BACK_BANKS = 3
 MEAN_BEHIND_TILE = 2
 VAR_BEHIND_TILE = 4
 SCALE_BEHIND_TILE = 6
-VECTOR_TILES = 1
+VECTOR_TILES = 0
 W_RUN_PASSES = 4
 GPSIMD_W_RUNS = 3
 

@@ -18,41 +18,62 @@ N_OUT = 64
 PACK = 4
 K_PASS = P * PACK
 EPS = 1e-8
-
-GROUP_BINS = ((0, 16384, 1024), (16384, 32768, 2048), (32768, 65536, 4096))
-
-UNIT_BINS = 4096
-UNITS = 65536 // UNIT_BINS
-PART_PASSES = UNIT_BINS // K_PASS
-BANK_PASSES = 4
-PIECE_PASSES = 2
-UNIT_PIECES = 2 * PART_PASSES // PIECE_PASSES
-PIECE_COUNT = 256
-DOUBLE_PASSES = 2 * PART_PASSES
-UNIT_BANKS = 2 * PART_PASSES // BANK_PASSES
-TILE_PASSES = 2
-UNIT_TILES = 2 * PART_PASSES // TILE_PASSES
-BACK_BANKS = 3
-
-MEAN_BEHIND_TILE = 2
-VAR_BEHIND_TILE = 4
-SCALE_BEHIND_TILE = 6
-VECTOR_TILES = 0
-W_RUN_PASSES = 4
-GPSIMD_W_RUNS = 3
-
 FLOPS = 2 * 131072 * T * N_OUT
 
+GROUP_BINS = ((0, 16384, 1024), (16384, 32768, 2048), (32768, 65536, 4096))
+GROUP_BASE_PASS = (0, 64, 128)
 
-def group_of_unit(u):
-    for gi, (first_bin, end_bin, band_bins) in enumerate(GROUP_BINS):
-        if first_bin <= u * UNIT_BINS < end_bin:
-            return gi
-    raise ValueError("no such unit")
+TILE_PASSES = 8
+SLOTS = 4
+PIECE_COUNT = 256
+
+GRANULES = [
+    (gi, pair, quarter)
+    for gi, (first_bin, end_bin, band_bins) in enumerate(GROUP_BINS)
+    for pair in range((end_bin - first_bin) // (2 * band_bins))
+    for quarter in range(2 * band_bins // K_PASS // SLOTS)
+]
+N_G = len(GRANULES)
+
+BATCHES = [[0], [1], [2], [3, 4], [5, 6, 7]] + [list(range(g, g + 4)) for g in range(8, N_G, 4)]
+QUAD = 4
+PROLOGUE = 3
+LEAD = 6
+X_AHEAD = 10
+W_AHEAD = 4
+GPSIMD_W_SLOTS = (4, 2)
 
 
-def half_passes_of_unit(u):
-    return GROUP_BINS[group_of_unit(u)][2] // K_PASS
+def half_passes(gi):
+    return GROUP_BINS[gi][2] // K_PASS
+
+
+def x_places(g, side):
+    gi, pair, quarter = GRANULES[g]
+    half = half_passes(gi)
+    places = []
+    for c in range(SLOTS * quarter, SLOTS * quarter + SLOTS):
+        at = GROUP_BINS[gi][0] // K_PASS + (2 * pair + side) * half + c % half
+        places.append((c // half, at // TILE_PASSES, at % TILE_PASSES))
+    return places
+
+
+def w_place(g, side):
+    gi, pair, quarter = GRANULES[g]
+    at = (2 * pair + side) * 2 * half_passes(gi) + SLOTS * quarter
+    return gi, at // TILE_PASSES, at % TILE_PASSES
+
+
+def in_order(keys):
+    seen = []
+    for key in keys:
+        if key not in seen:
+            seen.append(key)
+    return seen
+
+
+X_LOADS = in_order([place[:2] for g in range(N_G) for side in range(2) for place in x_places(g, side)])
+W_LOADS = in_order([w_place(g, side)[:2] for g in range(N_G) for side in range(2)])
 
 
 def tile_bandsplitmodule_k_kernel(
@@ -65,46 +86,55 @@ def tile_bandsplitmodule_k_kernel(
     with ExitStack() as stack:
         const = stack.enter_context(tc.tile_pool(name="const", bufs=1))
         setup = stack.enter_context(tc.tile_pool(name="setup", bufs=1))
-        xk_pool = stack.enter_context(tc.tile_pool(name="xk", bufs=6))
+        xk_pool = stack.enter_context(tc.tile_pool(name="xk", bufs=12))
+        wk_pool = stack.enter_context(tc.tile_pool(name="wk", bufs=6))
         xh_pool = stack.enter_context(tc.tile_pool(name="xh", bufs=6))
         y_pool = stack.enter_context(tc.tile_pool(name="y", bufs=3))
-        gx_pool = stack.enter_context(tc.tile_pool(name="gx", bufs=3))
-        xq_pool = stack.enter_context(tc.tile_pool(name="xq", bufs=2))
-        wk_pool = stack.enter_context(tc.tile_pool(name="wk", bufs=2))
+        gx_pool = stack.enter_context(tc.tile_pool(name="gx", bufs=2))
         gw_pool = stack.enter_context(tc.tile_pool(name="gw", bufs=1))
-        wq_pool = stack.enter_context(tc.tile_pool(name="wq", bufs=2))
+        xq_pool = stack.enter_context(tc.tile_pool(name="xq", bufs=8))
+        wq_pool = stack.enter_context(tc.tile_pool(name="wq", bufs=9))
         small = stack.enter_context(tc.tile_pool(name="small", bufs=3))
-        ring = stack.enter_context(tc.psum_pool(name="ring", bufs=4))
-        back = stack.enter_context(tc.psum_pool(name="back", bufs=BACK_BANKS))
-        fold_ps = stack.enter_context(tc.psum_pool(name="fold_ps", bufs=1))
+        count_ps = stack.enter_context(tc.psum_pool(name="count_ps", bufs=2))
+        norm_ps = stack.enter_context(tc.psum_pool(name="norm_ps", bufs=2))
+        back_ps = stack.enter_context(tc.psum_pool(name="back_ps", bufs=3))
+        misc_ps = stack.enter_context(tc.psum_pool(name="misc_ps", bufs=1))
         stack.enter_context(tc.manual_schedule())
 
-        def load_x(u):
-            tiles = []
-            for x_part in (x_real, x_imag):
-                xk = xk_pool.tile([P, PART_PASSES, PACK * T], BF16)
-                rows = x_part[0, u * UNIT_BINS : (u + 1) * UNIT_BINS, :]
-                nc.sync.dma_start(out=xk[:], in_=rows.rearrange("(s p j) t -> p s (j t)", p=P, j=PACK))
-                tiles.append(xk)
-            return tiles
+        x_tiles = {}
+        w_tiles = {}
 
-        def load_w(d):
-            gi = group_of_unit(2 * d)
-            first_double = GROUP_BINS[gi][0] // (2 * UNIT_BINS)
-            rows = weights[gi].rearrange("k c n -> (k c) n")
-            wk = wk_pool.tile([P, 2 * DOUBLE_PASSES, PACK * N_OUT], BF16)
-            for a in range(4):
-                first = ((d - first_double) * 4 + a) * PART_PASSES * K_PASS
-                nc.sync.dma_start(
-                    out=wk[:, a * PART_PASSES : (a + 1) * PART_PASSES, :],
-                    in_=rows[first : first + PART_PASSES * K_PASS, :].rearrange(
-                        "(s p j) n -> p s (j n)", p=P, j=PACK
-                    ),
-                )
-            return wk
+        def load_x(n, first=0, count=TILE_PASSES):
+            if n >= len(X_LOADS):
+                return
+            part, at = X_LOADS[n]
+            if (part, at) not in x_tiles:
+                xk = xk_pool.tile([P, TILE_PASSES, PACK * T], BF16)
+                x_tiles[part, at] = xk
+            row = (at * TILE_PASSES + first) * K_PASS
+            rows = (x_real, x_imag)[part][0, row : row + count * K_PASS, :]
+            nc.sync.dma_start(
+                out=x_tiles[part, at][:, first : first + count, :],
+                in_=rows.rearrange("(s p j) t -> p s (j t)", p=P, j=PACK),
+            )
 
-        x_tiles = {0: load_x(0), 1: load_x(1)}
-        w_tiles = {0: load_w(0)}
+        def load_w(n):
+            if n >= len(W_LOADS):
+                return
+            gi, at = W_LOADS[n]
+            wk = wk_pool.tile([P, TILE_PASSES, PACK * N_OUT], BF16)
+            w_tiles[gi, at] = wk
+            row = at * TILE_PASSES * K_PASS
+            rows = weights[gi].rearrange("k c n -> (k c) n")[row : row + TILE_PASSES * K_PASS, :]
+            nc.sync.dma_start(out=wk[:], in_=rows.rearrange("(s p j) n -> p s (j n)", p=P, j=PACK))
+
+        for first in (0, SLOTS):
+            for n in range(2):
+                load_x(n, first, SLOTS)
+        for n in range(W_AHEAD):
+            load_w(n)
+            load_x(2 * n + 2)
+            load_x(2 * n + 3)
 
         ident = const.tile([P, P], F32)
         make_identity(nc, ident[:])
@@ -123,23 +153,19 @@ def tile_bandsplitmodule_k_kernel(
             )
             folds.append(fold)
 
+        one = const.tile([P, 1], F32)
+        nc.vector.memset(one[:], 1.0)
+        eps = const.tile([P, 1], F32)
+        nc.vector.tensor_scalar(out=eps[:], in0=one[:], scalar1=EPS, scalar2=None, op0=ALU.mult)
+        warm = const.tile([P, 1], F32)
+        nc.scalar.activation(out=warm[:], in_=one[:], func=ACT.Sqrt)
+
         def load_channel_vector(v16, v32, v64, name):
             nat = setup.tile([P, 2 * K_PASS], BF16, name=name + "_nat")
             nc.scalar.dma_start(out=nat[0:32, :], in_=v16.rearrange("k (a c) -> (k a) c", c=2 * K_PASS))
             nc.scalar.dma_start(out=nat[32:64, :], in_=v32.rearrange("k (a c) -> (k a) c", c=2 * K_PASS))
             nc.scalar.dma_start(out=nat[64:128, :], in_=v64.rearrange("k (a c) -> (k a) c", c=2 * K_PASS))
             return nat
-
-        def sort_channel_vector(nat, name):
-            perm = setup.tile([P, 2, PACK, P], F32, name=name + "_perm")
-            nc.vector.tensor_copy(out=perm[:], in_=nat[:].rearrange("q (c p j) -> q c j p", c=2, j=PACK))
-            return perm
-
-        def turn_channel_vector(perm, c):
-            turned = back.tile([P, PACK, P], F32, tag="xb", name="turned")
-            for j in range(PACK):
-                nc.tensor.transpose(out=turned[:, j, :], in_=perm[:, c, j, :], identity=ident[:])
-            return turned
 
         gain_nat = load_channel_vector(g16, g32, g64, "gain")
         shift_nat = load_channel_vector(b16, b32, b64, "shift")
@@ -155,258 +181,297 @@ def tile_bandsplitmodule_k_kernel(
         nc.scalar.dma_start(out=c_nat[12:16, :], in_=c64.rearrange("(g a) n -> g (a n)", a=2))
         bias = const.tile([P, P], F32)
 
-        one = const.tile([P, 1], F32)
-        nc.vector.memset(one[:], 1.0)
-        warm = const.tile([P, 1], F32)
-        nc.scalar.activation(out=warm[:], in_=one[:], func=ACT.Sqrt)
-
         result = const.tile([P, 16, 2 * T], F32)
 
-        banks = [(part, kb) for part in range(2) for kb in range(PART_PASSES // BANK_PASSES)]
-        xts = {}
-        xhs = {}
-        ys = {}
+        def sort_channel_vector(nat, name):
+            perm = setup.tile([P, 2, PACK, P], F32, name=name + "_perm")
+            nc.scalar.copy(out=perm[:], in_=nat[:].rearrange("q (c p j) -> q c j p", c=2, j=PACK))
+            return perm
+
+        def turn_channel_vector(perm, cols):
+            for c in range(2):
+                turned = back_ps.tile([P, PACK, P], F32, tag="xb", name="turned")
+                for j in range(PACK):
+                    nc.tensor.transpose(out=turned[:, j, :], in_=perm[:, c, j, :], identity=ident[:])
+                nc.scalar.copy(out=cols[:, :, c, :], in_=turned[:].rearrange("p j q -> p q j"))
+
+        def prepare_bias():
+            c_f32 = setup.tile([P, P], F32)
+            nc.scalar.copy(out=c_f32[:], in_=c_nat[:])
+            c_turned = back_ps.tile([P, P], F32, tag="xb")
+            nc.tensor.transpose(out=c_turned[:], in_=c_f32[:], identity=ident[:])
+            nc.scalar.copy(out=bias[:], in_=c_turned[:])
+
+        def words(g, side):
+            return [x_tiles[part, at][:, i, :].bitcast(F32) for part, at, i in x_places(g, side)]
+
+        def transpose_side(pool, g, side, name):
+            xt = pool.tile([P, SLOTS, P], F32, tag=name, name=name)
+            for a, view in enumerate(words(g, side)):
+                nc.tensor.transpose(out=xt[:, a, :], in_=view, identity=ident[:])
+            return xt
+
+        counted = {}
         st = {}
+        batch_of = {g: b for b, batch in enumerate(BATCHES) for g in batch}
+
+        def batch_shape(b):
+            gi = GRANULES[BATCHES[b][0]][0]
+            pieces = half_passes(gi)
+            return gi, SLOTS * len(BATCHES[b]) // pieces, pieces
+
+        def count_transpose(g):
+            if g < N_G:
+                for side in range(2):
+                    counted[g, side] = transpose_side(count_ps, g, side, "xc")
+
+        def count(g, side):
+            b = batch_of[g]
+            gi, bands, pieces = batch_shape(b)
+            if g == BATCHES[b][0] and side == 0:
+                stats = small.tile([P, bands, pieces, 6], F32)
+                st[b, "stats"] = stats
+            band = 2 * (GRANULES[g][1] - GRANULES[BATCHES[b][0]][1]) + side
+            bank = counted[g, side][:].rearrange("p s m -> p (s m)")
+            for h in range(2):
+                nc.vector.bn_stats(
+                    out=st[b, "stats"][:, band, 2 * GRANULES[g][2] + h, :],
+                    in_=bank[:, h * 2 * P : (h + 1) * 2 * P].bitcast(BF16),
+                )
+
+        def fields_of(b):
+            fields = st[b, "stats"][:].rearrange("p b k (e f) -> p b k e f", f=3)
+            return fields[:, :, :, :, 1], fields[:, :, :, :, 2]
+
+        def fold_mean(b):
+            gi, bands, pieces = batch_shape(b)
+            mean_ps = misc_ps.tile([P, bands * pieces * 2], F32, tag="misc")
+            nc.tensor.matmul(
+                out=mean_ps[:], lhsT=folds[gi][:].rearrange("p b m -> p (b m)"),
+                rhs=fields_of(b)[0].rearrange("p b k e -> p (b k e)"), start=True, stop=True,
+            )
+            st[b, "mean_ps"] = mean_ps
+
+        def mean_step(b):
+            gi, bands, pieces = batch_shape(b)
+            neg_mean = small.tile([P, bands, 2], F32)
+            nc.vector.tensor_reduce(
+                out=neg_mean[:], in_=st[b, "mean_ps"][:].rearrange("p (b k e) -> p b e k", b=bands, e=2),
+                axis=AX.X, op=ALU.add, negate=True,
+            )
+            st[b, "neg_mean"] = neg_mean
+
+        def deviation_step(b):
+            gi, bands, pieces = batch_shape(b)
+            dev = small.tile([P, bands, pieces, 2], F32)
+            nc.vector.tensor_tensor(
+                out=dev[:], in0=fields_of(b)[0],
+                in1=st[b, "neg_mean"][:].unsqueeze(2).to_broadcast([P, bands, pieces, 2]), op=ALU.add,
+            )
+            st[b, "dev"] = dev
+
+        def square_step(b):
+            gi, bands, pieces = batch_shape(b)
+            dev_sq = small.tile([P, bands, pieces, 2], F32)
+            nc.vector.tensor_tensor(out=dev_sq[:], in0=st[b, "dev"][:], in1=st[b, "dev"][:], op=ALU.mult)
+            st[b, "dev_sq"] = dev_sq
+
+        def spread_step(b):
+            gi, bands, pieces = batch_shape(b)
+            spread = small.tile([P, bands, pieces, 2], F32)
+            nc.vector.scalar_tensor_tensor(
+                out=spread[:], in0=fields_of(b)[1], scalar=1.0 / PIECE_COUNT, in1=st[b, "dev_sq"][:],
+                op0=ALU.mult, op1=ALU.add,
+            )
+            st[b, "spread"] = spread
+
+        def fold_var(b):
+            gi, bands, pieces = batch_shape(b)
+            var_ps = misc_ps.tile([P, bands * pieces * 2], F32, tag="misc")
+            nc.tensor.matmul(
+                out=var_ps[:], lhsT=folds[gi][:].rearrange("p b m -> p (b m)"),
+                rhs=st[b, "spread"][:].rearrange("p b k e -> p (b k e)"), start=True, stop=True,
+            )
+            st[b, "var_ps"] = var_ps
+
+        def var_step(b):
+            gi, bands, pieces = batch_shape(b)
+            var = small.tile([P, bands, 2], F32)
+            nc.vector.tensor_reduce(
+                out=var[:], in_=st[b, "var_ps"][:].rearrange("p (b k e) -> p b e k", b=bands, e=2),
+                axis=AX.X, op=ALU.add,
+            )
+            st[b, "var"] = var
+
+        def std_step(b):
+            gi, bands, pieces = batch_shape(b)
+            std = small.tile([P, bands, 2], F32)
+            nc.scalar.activation(out=std[:], in_=st[b, "var"][:], func=ACT.Sqrt, bias=eps[:])
+            st[b, "std"] = std
+
+        def rstd_step(b):
+            gi, bands, pieces = batch_shape(b)
+            rstd = small.tile([P, bands, 2], F32)
+            nc.vector.reciprocal(out=rstd[:], in_=st[b, "std"][:])
+            st[b, "rstd"] = rstd
+
+        def offset_step(b):
+            gi, bands, pieces = batch_shape(b)
+            offset = small.tile([P, bands, 2], F32)
+            nc.vector.tensor_tensor(out=offset[:], in0=st[b, "neg_mean"][:], in1=st[b, "rstd"][:], op=ALU.mult)
+            st[b, "offset"] = offset
+
+        turned_x = {}
+        xhs = {}
+        xbs = {}
+        ys = {}
+        gxs = {}
+        gws = {}
         xqs = {}
         wqs = {}
 
-        def transpose_and_count(u, n):
-            part, kb = banks[n]
-            half = half_passes_of_unit(u)
-            xk = x_tiles[u][part]
-            if n == 0:
-                stats = small.tile([P, UNIT_PIECES, 6], F32)
-                st[u, "stats"] = stats
-            xt = ring.tile([P, BANK_PASSES * P], F32)
-            for a in range(BANK_PASSES):
-                nc.tensor.transpose(
-                    out=xt[:, a * P : (a + 1) * P],
-                    in_=xk[:, kb * BANK_PASSES + a, :].bitcast(F32),
-                    identity=ident[:],
+        def norm_transpose(g, side):
+            if g < N_G:
+                turned_x[g, side] = transpose_side(norm_ps, g, side, "xt")
+
+        def normalise(g, side):
+            if g >= N_G:
+                return
+            b = batch_of[g]
+            band = 2 * (GRANULES[g][1] - GRANULES[BATCHES[b][0]][1]) + side
+            xh = xh_pool.tile([P, 2, SLOTS, P], F32)
+            halves = turned_x[g, side][:].rearrange("p s m -> p (s m)").bitcast(BF16)
+            halves = halves.rearrange("p (s w e) -> p s w e", s=SLOTS, e=2)
+            for e in range(2):
+                nc.scalar.activation(
+                    out=xh[:, e, :, :], in_=halves[:, :, :, e], func=ACT.Identity,
+                    bias=st[b, "offset"][:, band, e : e + 1], scale=st[b, "rstd"][:, band, e : e + 1],
                 )
-            for h in range(BANK_PASSES // PIECE_PASSES):
-                i = kb * BANK_PASSES + h * PIECE_PASSES
-                pieces_per_half = half // PIECE_PASSES
-                piece = (i // half) * 2 * pieces_per_half + part * pieces_per_half + (i % half) // PIECE_PASSES
-                nc.vector.bn_stats(
-                    out=st[u, "stats"][:, piece, :],
-                    in_=xt[:, h * PIECE_PASSES * P : (h + 1) * PIECE_PASSES * P].bitcast(BF16),
-                )
-            xts[u, n] = xt
+            xhs[g, side] = xh
 
-        def stats_mean(u, fill):
-            gi = group_of_unit(u)
-            bands = UNIT_BINS // GROUP_BINS[gi][2]
-            fields = st[u, "stats"][:].rearrange("p k (e f) -> p k e f", f=3)
-            means = fields[:, :, :, 1]
-            squares = fields[:, :, :, 2]
-            mean_ps = fold_ps.tile([P, 2 * UNIT_PIECES], F32, tag="fold")
-            nc.tensor.matmul(
-                out=mean_ps[:], lhsT=folds[gi][:].rearrange("p b m -> p (b m)"),
-                rhs=means.rearrange("p k e -> p (k e)"), start=True, stop=True,
-            )
-            inner = small.tile([P, UNIT_PIECES, 2], F32)
-            nc.vector.tensor_scalar(
-                out=inner[:], in0=squares, scalar1=1.0 / PIECE_COUNT, scalar2=EPS, op0=ALU.mult, op1=ALU.add
-            )
-            fill()
-            neg_mean = small.tile([P, bands, 2], F32)
-            nc.vector.tensor_reduce(
-                out=neg_mean[:], in_=mean_ps[:].rearrange("p (b k e) -> p b e k", b=bands, e=2),
-                axis=AX.X, op=ALU.add, negate=True,
-            )
-            dev = small.tile([P, UNIT_PIECES, 2], F32)
-            nc.vector.tensor_tensor(
-                out=dev[:].rearrange("p (b k) e -> p b k e", b=bands),
-                in0=means.rearrange("p (b k) e -> p b k e", b=bands),
-                in1=neg_mean[:].unsqueeze(2).to_broadcast([P, bands, UNIT_PIECES // bands, 2]),
-                op=ALU.add,
-            )
-            dev_sq = small.tile([P, UNIT_PIECES, 2], F32)
-            nc.vector.tensor_tensor(out=dev_sq[:], in0=dev[:], in1=dev[:], op=ALU.mult)
-            spread = small.tile([P, UNIT_PIECES, 2], F32)
-            nc.vector.tensor_tensor(out=spread[:], in0=dev_sq[:], in1=inner[:], op=ALU.add)
-            st[u, "neg_mean"] = neg_mean
-            st[u, "spread"] = spread
-
-        def stats_var(u, fill):
-            gi = group_of_unit(u)
-            bands = UNIT_BINS // GROUP_BINS[gi][2]
-            var_ps = fold_ps.tile([P, 2 * UNIT_PIECES], F32, tag="fold")
-            nc.tensor.matmul(
-                out=var_ps[:], lhsT=folds[gi][:].rearrange("p b m -> p (b m)"),
-                rhs=st[u, "spread"][:].rearrange("p k e -> p (k e)"), start=True, stop=True,
-            )
-            fill()
-            var = small.tile([P, bands, 2], F32)
-            nc.vector.tensor_reduce(
-                out=var[:], in_=var_ps[:].rearrange("p (b k e) -> p b e k", b=bands, e=2),
-                axis=AX.X, op=ALU.add,
-            )
-            st[u, "var"] = var
-
-        def stats_scale(u, fill):
-            bands = UNIT_BINS // GROUP_BINS[group_of_unit(u)][2]
-            std = small.tile([P, bands, 2], F32)
-            nc.scalar.activation(out=std[:], in_=st[u, "var"][:], func=ACT.Sqrt)
-            fill()
-            rstd = small.tile([P, bands, 2], F32)
-            nc.vector.reciprocal(out=rstd[:], in_=std[:])
-            offset = small.tile([P, bands, 2], F32)
-            nc.vector.tensor_tensor(out=offset[:], in0=st[u, "neg_mean"][:], in1=rstd[:], op=ALU.mult)
-            st[u, "rstd"] = rstd
-            st[u, "offset"] = offset
-
-        def normalise(u, n):
-            part, kb = banks[n]
-            half = half_passes_of_unit(u)
-            run = min(half, BANK_PASSES)
-            xh = xh_pool.tile([P, 2, BANK_PASSES, P], F32)
-            halves = xts[u, n][:].bitcast(BF16).rearrange("p (s w e) -> p s w e", s=BANK_PASSES, e=2)
-            for s0 in range(0, BANK_PASSES, run):
-                band = (kb * BANK_PASSES + s0) // half
+        def back_transpose(g, m):
+            if g >= N_G:
+                return
+            xb = back_ps.tile([P, 2, 2, P], F32, tag="xb")
+            for side in range(2):
                 for e in range(2):
-                    nc.scalar.activation(
-                        out=xh[:, e, s0 : s0 + run, :], in_=halves[:, s0 : s0 + run, :, e], func=ACT.Identity,
-                        bias=st[u, "offset"][:, band, e : e + 1], scale=st[u, "rstd"][:, band, e : e + 1],
-                    )
-            xhs[u, n] = xh
+                    nc.tensor.transpose(out=xb[:, side, e, :], in_=xhs[g, side][:, e, m, :], identity=ident[:])
+            xbs[g, m] = xb
 
-        xbs = {}
-
-        def back_transpose(u, m):
-            xh = xhs[u, m * TILE_PASSES // BANK_PASSES]
-            xb = back.tile([P, TILE_PASSES, 2, P], F32)
-            for a in range(TILE_PASSES):
-                for e in range(2):
-                    nc.tensor.transpose(
-                        out=xb[:, a, e, :], in_=xh[:, e, (m * TILE_PASSES + a) % BANK_PASSES, :], identity=ident[:]
-                    )
-            xbs[u, m] = xb
-
-        def gain_and_shift(u, m):
-            half = half_passes_of_unit(u)
-            part = m * TILE_PASSES // PART_PASSES
-            if m * TILE_PASSES % PART_PASSES == 0:
-                y = y_pool.tile([P, PACK, PART_PASSES, T], BF16)
-                ys[u, part] = y
-            for a in range(TILE_PASSES):
-                i = (m * TILE_PASSES + a) % PART_PASSES
-                row_pass = 2 * PART_PASSES * u + (i // half) * 2 * half + part * half + i % half
+        def gain_and_shift(g, m):
+            gi, pair, quarter = GRANULES[g]
+            if m == 0:
+                y = y_pool.tile([P, PACK, SLOTS, 2, T], BF16)
+                ys[g] = y
+            for side in range(2):
+                at = GROUP_BASE_PASS[gi] + (2 * pair + side) * 2 * half_passes(gi) + SLOTS * quarter + m
                 for j in range(PACK):
-                    col = row_pass * PACK + j
-                    dst = ys[u, part][:, j, i, :].rearrange("p (e w) -> p e w", e=2)
-                    src = xbs[u, m][:, a, :, 32 * j : 32 * (j + 1)]
-                    if m < VECTOR_TILES:
-                        nc.vector.tensor_scalar(
-                            out=dst, in0=src, scalar1=gain[:, col : col + 1], scalar2=shift[:, col : col + 1],
-                            op0=ALU.mult, op1=ALU.add,
-                        )
-                    else:
-                        nc.scalar.activation(
-                            out=dst, in_=src, func=ACT.Identity,
-                            bias=shift[:, col : col + 1], scale=gain[:, col : col + 1],
-                        )
-
-        gxs = {}
-
-        def regroup_x_part(u, part):
-            gx = gx_pool.tile([P, PART_PASSES, PACK * T], BF16, align_bytes=64)
-            nc.vector.tensor_copy(
-                out=gx[:].rearrange("p s (m i j) -> p (s m) j i", i=4, j=PACK),
-                in_=ys[u, part][:].rearrange("p j s (m i) -> p (s m) j i", i=4),
-            )
-            gxs[u, part] = gx
-
-        def quantise_x_part(u, part):
-            half = half_passes_of_unit(u)
-            bands = PART_PASSES // half
-            if u % 2 == 0 and part == 0:
-                xq = xq_pool.tile([P, DOUBLE_PASSES, 2 * T], U32, align_bytes=64)
-                xs = xq_pool.tile([P, DOUBLE_PASSES, 2 * T], U8, align_bytes=64)
-                xqs[u // 2] = (xq, xs)
-            xq, xs = xqs[u // 2]
-            gx = gxs[u, part]
-            for i in range(PART_PASSES):
-                band_in_double = (u % 2) * bands + i // half
-                pair, side = divmod(band_in_double, 2)
-                slot = pair * 2 * half + part * half + i % half
-                nc.vector.quantize_mx(
-                    out=xq[:, slot, side * T : (side + 1) * T].bitcast(FP8X4),
-                    scales=xs[:, slot, side * T : (side + 1) * T],
-                    in_=gx[:, i, :],
-                )
-
-        def quantise_x(u, part):
-            regroup_x_part(u, part)
-            quantise_x_part(u, part)
-
-        gws = {}
-
-        def regroup_w_runs(u):
-            half = half_passes_of_unit(u)
-            run = W_RUN_PASSES
-            first_slot = (u % 2) * PART_PASSES
-            runs = []
-            for slot in range(first_slot, first_slot + PART_PASSES, run):
-                for side in range(2):
-                    runs.append((slot // (2 * half) * 2 + side, slot % (2 * half), run))
-            return runs
-
-        def regroup_w(u, on_gpsimd, band_in_double, first_pass, run):
-            half = half_passes_of_unit(u)
-            pair, side = divmod(band_in_double, 2)
-            slot = pair * 2 * half + first_pass - (u % 2) * PART_PASSES
-            raw = band_in_double * 2 * half + first_pass
-            grouped = gws[u][:, slot : slot + run, side, :]
-            rows = w_tiles[u // 2][:, raw : raw + run, :]
-            if on_gpsimd:
-                nc.gpsimd.tensor_scalar(
-                    out=grouped.rearrange("p c (n j) -> p c n j", j=PACK),
-                    in0=rows.rearrange("p c (j n) -> p c n j", j=PACK),
-                    scalar1=1.0, scalar2=0.0, op0=ALU.mult, op1=ALU.add,
-                )
-            else:
-                nc.vector.tensor_copy(
-                    out=grouped.rearrange("p c (m i j) -> p c m j i", i=4, j=PACK),
-                    in_=rows.rearrange("p c (j m i) -> p c m j i", j=PACK, i=4),
-                )
-
-        def quantise_w(u):
-            if u % 2 == 0:
-                wq = wq_pool.tile([P, DOUBLE_PASSES, 2 * N_OUT], U32, align_bytes=64)
-                ws = wq_pool.tile([P, DOUBLE_PASSES, 2 * N_OUT], U8, align_bytes=64)
-                wqs[u // 2] = (wq, ws)
-            wq, ws = wqs[u // 2]
-            slots = slice((u % 2) * PART_PASSES, (u % 2 + 1) * PART_PASSES)
-            nc.vector.quantize_mx(
-                out=wq[:, slots, :].rearrange("p c m -> p (c m)").bitcast(FP8X4),
-                scales=ws[:, slots, :].rearrange("p c m -> p (c m)"),
-                in_=gws[u][:].rearrange("p c a m -> p (c a m)"),
-            )
-
-        def multiply_and_store(d):
-            half = half_passes_of_unit(2 * d)
-            pairs = DOUBLE_PASSES // (2 * half)
-            first_pair = sum(PART_PASSES // half_passes_of_unit(2 * dd) for dd in range(d))
-            wq, ws = wqs[d]
-            xq, xs = xqs[d]
-            acc = back.tile([P, pairs, 2 * T], F32, tag="xb")
-            for pair in range(pairs):
-                for c in range(2 * half):
-                    slot = pair * 2 * half + c
-                    nc.tensor.matmul_mx(
-                        out=acc[:, pair, :],
-                        lhsT=wq[:, slot, :].bitcast(FP8X4), lhsT_scale=ws[:, slot, :],
-                        rhs=xq[:, slot, :].bitcast(FP8X4), rhs_scale=xs[:, slot, :],
-                        start=(c == 0), stop=(c == 2 * half - 1),
+                    col = at * PACK + j
+                    nc.scalar.activation(
+                        out=ys[g][:, j, m, side, :].rearrange("p (e w) -> p e w", e=2),
+                        in_=xbs[g, m][:, side, :, 32 * j : 32 * (j + 1)], func=ACT.Identity,
+                        bias=shift[:, col : col + 1], scale=gain[:, col : col + 1],
                     )
+
+        def regroup_x(g, first=0, count=SLOTS):
+            if first == 0:
+                gx = gx_pool.tile([P, SLOTS, 2, PACK * T], BF16, align_bytes=64)
+                gxs[g] = gx
+            slots = slice(first, first + count)
+            nc.vector.tensor_copy(
+                out=gxs[g][:, slots, :, :].rearrange("p s a (m i j) -> p (s a m) j i", i=4, j=PACK),
+                in_=ys[g][:, :, slots, :, :].rearrange("p j s a (m i) -> p (s a m) j i", i=4),
+            )
+
+        def quantise_x(g, first=0, count=SLOTS):
+            if first == 0:
+                xq = xq_pool.tile([P, SLOTS, 2 * T], U32, align_bytes=64)
+                xs = xq_pool.tile([P, SLOTS, 2 * T], U8, align_bytes=64)
+                xqs[g] = (xq, xs)
+            xq, xs = xqs[g]
+            slots = slice(first, first + count)
+            nc.vector.quantize_mx(
+                out=xq[:, slots, :].rearrange("p s m -> p (s m)").bitcast(FP8X4),
+                scales=xs[:, slots, :].rearrange("p s m -> p (s m)"),
+                in_=gxs[g][:, slots, :, :].rearrange("p s a m -> p (s a m)"),
+            )
+
+        def regroup_w(g, on_gpsimd):
+            if g >= N_G:
+                return
+            if on_gpsimd:
+                gw = gw_pool.tile([P, SLOTS, 2, PACK * N_OUT], BF16, align_bytes=64)
+                gws[g] = gw
+            for side in range(2):
+                gi, at, i = w_place(g, side)
+                if on_gpsimd:
+                    first, last = 0, GPSIMD_W_SLOTS[side]
+                else:
+                    first, last = GPSIMD_W_SLOTS[side], SLOTS
+                if first == last:
+                    continue
+                grouped = gws[g][:, first:last, side, :]
+                rows = w_tiles[gi, at][:, i + first : i + last, :]
+                if on_gpsimd:
+                    nc.gpsimd.tensor_scalar(
+                        out=grouped.rearrange("p c (n j) -> p c n j", j=PACK),
+                        in0=rows.rearrange("p c (j n) -> p c n j", j=PACK),
+                        scalar1=1.0, scalar2=0.0, op0=ALU.mult, op1=ALU.add,
+                    )
+                else:
+                    nc.vector.tensor_copy(
+                        out=grouped.rearrange("p c (m i j) -> p c m j i", i=4, j=PACK),
+                        in_=rows.rearrange("p c (j m i) -> p c m j i", j=PACK, i=4),
+                    )
+
+        def quantise_w(g):
+            wq = wq_pool.tile([P, SLOTS, 2 * N_OUT], U32, align_bytes=64)
+            ws = wq_pool.tile([P, SLOTS, 2 * N_OUT], U8, align_bytes=64)
+            wqs[g] = (wq, ws)
+            nc.vector.quantize_mx(
+                out=wq[:].rearrange("p s m -> p (s m)").bitcast(FP8X4),
+                scales=ws[:].rearrange("p s m -> p (s m)"),
+                in_=gws[g][:].rearrange("p s a m -> p (s a m)"),
+            )
+
+        accs = {}
+
+        def quad_pairs(k):
+            gi, pair, quarter = GRANULES[k * QUAD]
+            per_pair = half_passes(gi) * 2 // SLOTS
+            pairs_before = sum((e - s) // (2 * w) for s, e, w in GROUP_BINS[:gi])
+            return pairs_before + pair, QUAD // per_pair
+
+        def multiply(k, granules):
+            first_pair, pairs = quad_pairs(k)
+            per_pair = QUAD // pairs
+            if granules[0] == k * QUAD:
+                acc = misc_ps.tile([P, pairs, 2 * T], F32, tag="misc")
+                accs[k] = acc
+            for g in granules:
+                wq, ws = wqs[g]
+                xq, xs = xqs[g]
+                n = g - k * QUAD
+                for m in range(SLOTS):
+                    nc.tensor.matmul_mx(
+                        out=accs[k][:, n // per_pair, :],
+                        lhsT=wq[:, m, :].bitcast(FP8X4), lhsT_scale=ws[:, m, :],
+                        rhs=xq[:, m, :].bitcast(FP8X4), rhs_scale=xs[:, m, :],
+                        start=(n % per_pair == 0 and m == 0),
+                        stop=(n % per_pair == per_pair - 1 and m == SLOTS - 1),
+                    )
+
+        def add_bias(k):
+            first_pair, pairs = quad_pairs(k)
             for pair in range(pairs):
                 nc.vector.tensor_scalar(
                     out=result[:, first_pair + pair, :].rearrange("p (a w e) -> p a w e", a=2, e=2),
-                    in0=acc[:, pair, :].rearrange("p (a e w) -> p a w e", a=2, e=2),
+                    in0=accs[k][:, pair, :].rearrange("p (a e w) -> p a w e", a=2, e=2),
                     scalar1=bias[:, first_pair + pair : first_pair + pair + 1], scalar2=None, op0=ALU.add,
                 )
+
+        def store(k):
+            first_pair, pairs = quad_pairs(k)
             by_side = out[0].rearrange("n (g a) t -> a n g t", a=2)
             for side in range(2):
                 nc.sync.dma_start(
@@ -414,81 +479,126 @@ def tile_bandsplitmodule_k_kernel(
                     in_=result[side * N_OUT : (side + 1) * N_OUT, first_pair : first_pair + pairs, side * T : (side + 1) * T],
                 )
 
-        def nothing():
-            return None
-
-        for n in range(UNIT_BANKS):
-            transpose_and_count(0, n)
-        stats_mean(0, nothing)
+        count_transpose(0)
+        regroup_w(0, True)
         gain_perm = sort_channel_vector(gain_nat, "gain")
-        stats_var(0, nothing)
         shift_perm = sort_channel_vector(shift_nat, "shift")
-        stats_scale(0, nothing)
-        for perm, cols in ((gain_perm, gain_cols), (shift_perm, shift_cols)):
-            for c in range(2):
-                turned = turn_channel_vector(perm, c)
-                nc.vector.tensor_copy(out=cols[:, :, c, :], in_=turned[:].rearrange("p j q -> p q j"))
-        c_f32 = setup.tile([P, P], F32)
-        nc.vector.tensor_copy(out=c_f32[:], in_=c_nat[:])
-        c_turned = back.tile([P, P], F32, tag="xb")
-        nc.tensor.transpose(out=c_turned[:], in_=c_f32[:], identity=ident[:])
-        nc.vector.tensor_copy(out=bias[:], in_=c_turned[:])
+        for side in range(2):
+            count(0, side)
+        count_transpose(1)
+        for side in range(2):
+            norm_transpose(0, side)
+        fold_mean(0)
+        count(1, 0)
+        mean_step(0)
+        deviation_step(0)
+        square_step(0)
+        spread_step(0)
+        fold_var(0)
+        turn_channel_vector(gain_perm, gain_cols)
+        count(1, 1)
+        var_step(0)
+        std_step(0)
+        count_transpose(2)
+        fold_mean(1)
+        turn_channel_vector(shift_perm, shift_cols)
+        count(2, 0)
+        rstd_step(0)
+        offset_step(0)
+        for side in range(2):
+            normalise(0, side)
+            norm_transpose(1, side)
+        for m in range(2):
+            back_transpose(0, m)
+        mean_step(1)
+        deviation_step(1)
+        square_step(1)
+        spread_step(1)
+        fold_var(1)
+        count(2, 1)
+        var_step(1)
+        std_step(1)
+        count_transpose(3)
+        fold_mean(2)
+        rstd_step(1)
+        offset_step(1)
+        mean_step(2)
+        deviation_step(2)
+        square_step(2)
+        spread_step(2)
+        fold_var(2)
 
-        for u in range(UNITS):
-            more = u + 1 < UNITS
-            if u + 2 < UNITS:
-                x_tiles[u + 2] = load_x(u + 2)
-            if u % 2 == 0 and u // 2 + 1 < UNITS // 2:
-                w_tiles[u // 2 + 1] = load_w(u // 2 + 1)
-            if u >= 1:
-                quantise_x(u - 1, 1)
-                quantise_w(u - 1)
-            if u >= 3 and u % 2 == 1:
-                multiply_and_store((u - 3) // 2)
+        counted_to = PROLOGUE
+        spreading = [2]
+        for i in range(N_G):
+            load_x(i + X_AHEAD)
+            load_w(i + W_AHEAD)
+            if i % QUAD == 3 and i >= 7:
+                store(i // QUAD - 1)
 
-            gw = gw_pool.tile([P, PART_PASSES, 2, PACK * N_OUT], BF16, align_bytes=64)
-            gws[u] = gw
-            runs = regroup_w_runs(u)
-            for r in range(GPSIMD_W_RUNS):
-                regroup_w(u, True, *runs[r])
+            fresh = list(range(counted_to, min(i + 1 + min(LEAD, i + 4), N_G)))
+            counted_to += len(fresh)
+            finished = [b for b, batch in enumerate(BATCHES) if batch[-1] in fresh]
 
-            for n in range(UNIT_BANKS):
-                normalise(u, n)
-                if more:
-                    transpose_and_count(u + 1, n)
-                for m in range(BACK_BANKS):
-                    if m * TILE_PASSES // BANK_PASSES == n:
-                        back_transpose(u, m)
-                        if m < VECTOR_TILES:
-                            gain_and_shift(u, m)
-            for m in range(VECTOR_TILES):
-                back_transpose(u, m + BACK_BANKS)
+            back_transpose(i, 2)
+            normalise(i + 1, 0)
+            norm_transpose(i + 2, 0)
+            gain_and_shift(i, 0)
+            back_transpose(i, 3)
+            if fresh:
+                count(fresh[0], 0)
+            for b in spreading:
+                var_step(b)
+                std_step(b)
+            for g in fresh:
+                if g != fresh[0]:
+                    count(g, 0)
+                count(g, 1)
+                count_transpose(g + 1)
+            for b in spreading:
+                rstd_step(b)
+            for b in finished:
+                fold_mean(b)
+            if i % QUAD == 2 and i >= 6:
+                multiply(i // QUAD - 1, list(range(i - 6, i - 2)))
+            gain_and_shift(i, 1)
+            normalise(i + 1, 1)
+            norm_transpose(i + 2, 1)
+            gain_and_shift(i, 2)
+            back_transpose(i + 1, 0)
+            gain_and_shift(i, 3)
+            back_transpose(i + 1, 1)
 
-            def regroup_rest():
-                for r in range(GPSIMD_W_RUNS, len(runs)):
-                    regroup_w(u, False, *runs[r])
+            if i >= 1:
+                regroup_x(i - 1)
+            for b in spreading:
+                offset_step(b)
+            for b in finished:
+                mean_step(b)
+            regroup_w(i, False)
+            for b in finished:
+                deviation_step(b)
+            if i >= 1:
+                quantise_x(i - 1)
+            for b in finished:
+                square_step(b)
+            quantise_w(i)
+            regroup_w(i + 1, True)
+            for b in finished:
+                spread_step(b)
+                fold_var(b)
+            if i % QUAD == 2 and i >= 6:
+                add_bias(i // QUAD - 1)
+            if i == 2:
+                prepare_bias()
+            spreading = finished
 
-            def regroup_x():
-                regroup_x_part(u, 0)
-
-            def quantise_x_real():
-                quantise_x_part(u, 0)
-
-            for m in range(VECTOR_TILES, UNIT_TILES):
-                gain_and_shift(u, m)
-                if m + BACK_BANKS < UNIT_TILES:
-                    back_transpose(u, m + BACK_BANKS)
-                if more and m == MEAN_BEHIND_TILE:
-                    stats_mean(u + 1, regroup_rest)
-                if more and m == VAR_BEHIND_TILE:
-                    stats_var(u + 1, regroup_x)
-                if more and m == SCALE_BEHIND_TILE:
-                    stats_scale(u + 1, quantise_x_real)
-            if not more:
-                regroup_rest()
-                regroup_x()
-                quantise_x_real()
-
-        quantise_x(UNITS - 1, 1)
-        quantise_w(UNITS - 1)
-        multiply_and_store(UNITS // 2 - 1)
+        last = N_G // QUAD - 1
+        multiply(last, list(range(last * QUAD, N_G - 1)))
+        for first in (0, 2):
+            regroup_x(N_G - 1, first, 2)
+        for first in (0, 2):
+            quantise_x(N_G - 1, first, 2)
+        multiply(last, [N_G - 1])
+        add_bias(last)
+        store(last)

from contextlib import ExitStack

import concourse.mybir as mybir
from concourse.masks import make_identity

F32 = mybir.dt.float32
BF16 = mybir.dt.bfloat16
U32 = mybir.dt.uint32
U8 = mybir.dt.uint8
FP8X4 = mybir.dt.float8_e4m3fn_x4
ALU = mybir.AluOpType
ACT = mybir.ActivationFunctionType
AX = mybir.AxisListType

P = 128
T = 64
N_OUT = 64
PACK = 4
K_PASS = P * PACK
EPS = 1e-8
FLOPS = 2 * 131072 * T * N_OUT

GROUP_BINS = ((0, 16384, 1024), (16384, 32768, 2048), (32768, 65536, 4096))
GROUP_BASE_PASS = (0, 64, 128)

TILE_PASSES = 8
SLOTS = 4
PIECE_COUNT = 256

GRANULES = [
    (gi, pair, quarter)
    for gi, (first_bin, end_bin, band_bins) in enumerate(GROUP_BINS)
    for pair in range((end_bin - first_bin) // (2 * band_bins))
    for quarter in range(2 * band_bins // K_PASS // SLOTS)
]
N_G = len(GRANULES)

BATCHES = [[0], [1], [2], [3, 4], [5, 6, 7]] + [list(range(g, g + 4)) for g in range(8, N_G, 4)]
QUAD = 4
PROLOGUE = 3
LEAD = 6
X_AHEAD = 10
W_AHEAD = 4
GPSIMD_W_SLOTS = (4, 2)


def half_passes(gi):
    return GROUP_BINS[gi][2] // K_PASS


def x_places(g, side):
    gi, pair, quarter = GRANULES[g]
    half = half_passes(gi)
    places = []
    for c in range(SLOTS * quarter, SLOTS * quarter + SLOTS):
        at = GROUP_BINS[gi][0] // K_PASS + (2 * pair + side) * half + c % half
        places.append((c // half, at // TILE_PASSES, at % TILE_PASSES))
    return places


def w_place(g, side):
    gi, pair, quarter = GRANULES[g]
    at = (2 * pair + side) * 2 * half_passes(gi) + SLOTS * quarter
    return gi, at // TILE_PASSES, at % TILE_PASSES


def in_order(keys):
    seen = []
    for key in keys:
        if key not in seen:
            seen.append(key)
    return seen


X_LOADS = in_order([place[:2] for g in range(N_G) for side in range(2) for place in x_places(g, side)])
W_LOADS = in_order([w_place(g, side)[:2] for g in range(N_G) for side in range(2)])


def tile_bandsplitmodule_k_kernel(
    tc, x_real, x_imag, sample_rate,
    g16, b16, W16, c16, g32, b32, W32, c32, g64, b64, W64, c64, out,
):
    nc = tc.nc
    weights = (W16, W32, W64)

    with ExitStack() as stack:
        const = stack.enter_context(tc.tile_pool(name="const", bufs=1))
        setup = stack.enter_context(tc.tile_pool(name="setup", bufs=1))
        xk_pool = stack.enter_context(tc.tile_pool(name="xk", bufs=12))
        wk_pool = stack.enter_context(tc.tile_pool(name="wk", bufs=6))
        xh_pool = stack.enter_context(tc.tile_pool(name="xh", bufs=6))
        y_pool = stack.enter_context(tc.tile_pool(name="y", bufs=3))
        gx_pool = stack.enter_context(tc.tile_pool(name="gx", bufs=2))
        gw_pool = stack.enter_context(tc.tile_pool(name="gw", bufs=1))
        xq_pool = stack.enter_context(tc.tile_pool(name="xq", bufs=8))
        wq_pool = stack.enter_context(tc.tile_pool(name="wq", bufs=9))
        small = stack.enter_context(tc.tile_pool(name="small", bufs=3))
        count_ps = stack.enter_context(tc.psum_pool(name="count_ps", bufs=2))
        norm_ps = stack.enter_context(tc.psum_pool(name="norm_ps", bufs=2))
        back_ps = stack.enter_context(tc.psum_pool(name="back_ps", bufs=3))
        misc_ps = stack.enter_context(tc.psum_pool(name="misc_ps", bufs=1))
        stack.enter_context(tc.manual_schedule())

        x_tiles = {}
        w_tiles = {}

        def load_x(n, first=0, count=TILE_PASSES):
            if n >= len(X_LOADS):
                return
            part, at = X_LOADS[n]
            if (part, at) not in x_tiles:
                xk = xk_pool.tile([P, TILE_PASSES, PACK * T], BF16)
                x_tiles[part, at] = xk
            row = (at * TILE_PASSES + first) * K_PASS
            rows = (x_real, x_imag)[part][0, row : row + count * K_PASS, :]
            nc.sync.dma_start(
                out=x_tiles[part, at][:, first : first + count, :],
                in_=rows.rearrange("(s p j) t -> p s (j t)", p=P, j=PACK),
            )

        def load_w(n):
            if n >= len(W_LOADS):
                return
            gi, at = W_LOADS[n]
            wk = wk_pool.tile([P, TILE_PASSES, PACK * N_OUT], BF16)
            w_tiles[gi, at] = wk
            row = at * TILE_PASSES * K_PASS
            rows = weights[gi].rearrange("k c n -> (k c) n")[row : row + TILE_PASSES * K_PASS, :]
            nc.sync.dma_start(out=wk[:], in_=rows.rearrange("(s p j) n -> p s (j n)", p=P, j=PACK))

        for first in (0, SLOTS):
            for n in range(2):
                load_x(n, first, SLOTS)
        for n in range(W_AHEAD):
            load_w(n)
            load_x(2 * n + 2)
            load_x(2 * n + 3)

        ident = const.tile([P, P], F32)
        make_identity(nc, ident[:])

        eye32 = setup.tile([P, 32], F32)
        nc.vector.tensor_reduce(
            out=eye32[:], in_=ident[:].rearrange("p (b m) -> p m b", b=4), axis=AX.X, op=ALU.add
        )
        folds = []
        for gi, (first_bin, end_bin, band_bins) in enumerate(GROUP_BINS):
            results = 2 * band_bins // PIECE_COUNT
            fold = const.tile([P, 4, 32], F32, name="fold%d" % gi)
            nc.vector.tensor_scalar(
                out=fold[:], in0=eye32[:].unsqueeze(1).to_broadcast([P, 4, 32]),
                scalar1=1.0 / results, scalar2=None, op0=ALU.mult,
            )
            folds.append(fold)

        one = const.tile([P, 1], F32)
        nc.vector.memset(one[:], 1.0)
        eps = const.tile([P, 1], F32)
        nc.vector.tensor_scalar(out=eps[:], in0=one[:], scalar1=EPS, scalar2=None, op0=ALU.mult)
        warm = const.tile([P, 1], F32)
        nc.scalar.activation(out=warm[:], in_=one[:], func=ACT.Sqrt)

        def load_channel_vector(v16, v32, v64, name):
            nat = setup.tile([P, 2 * K_PASS], BF16, name=name + "_nat")
            nc.scalar.dma_start(out=nat[0:32, :], in_=v16.rearrange("k (a c) -> (k a) c", c=2 * K_PASS))
            nc.scalar.dma_start(out=nat[32:64, :], in_=v32.rearrange("k (a c) -> (k a) c", c=2 * K_PASS))
            nc.scalar.dma_start(out=nat[64:128, :], in_=v64.rearrange("k (a c) -> (k a) c", c=2 * K_PASS))
            return nat

        gain_nat = load_channel_vector(g16, g32, g64, "gain")
        shift_nat = load_channel_vector(b16, b32, b64, "shift")
        gain_cols = const.tile([P, P, 2, PACK], F32)
        shift_cols = const.tile([P, P, 2, PACK], F32)
        gain = gain_cols[:].rearrange("p q c j -> p (q c j)")
        shift = shift_cols[:].rearrange("p q c j -> p (q c j)")

        c_nat = setup.tile([P, P], BF16)
        nc.vector.memset(c_nat[:], 0.0)
        nc.scalar.dma_start(out=c_nat[0:8, :], in_=c16.rearrange("(g a) n -> g (a n)", a=2))
        nc.scalar.dma_start(out=c_nat[8:12, :], in_=c32.rearrange("(g a) n -> g (a n)", a=2))
        nc.scalar.dma_start(out=c_nat[12:16, :], in_=c64.rearrange("(g a) n -> g (a n)", a=2))
        bias = const.tile([P, P], F32)

        result = const.tile([P, 16, 2 * T], F32)

        def sort_channel_vector(nat, name):
            perm = setup.tile([P, 2, PACK, P], F32, name=name + "_perm")
            nc.scalar.copy(out=perm[:], in_=nat[:].rearrange("q (c p j) -> q c j p", c=2, j=PACK))
            return perm

        def turn_channel_vector(perm, cols):
            for c in range(2):
                turned = back_ps.tile([P, PACK, P], F32, tag="xb", name="turned")
                for j in range(PACK):
                    nc.tensor.transpose(out=turned[:, j, :], in_=perm[:, c, j, :], identity=ident[:])
                nc.scalar.copy(out=cols[:, :, c, :], in_=turned[:].rearrange("p j q -> p q j"))

        def prepare_bias():
            c_f32 = setup.tile([P, P], F32)
            nc.scalar.copy(out=c_f32[:], in_=c_nat[:])
            c_turned = back_ps.tile([P, P], F32, tag="xb")
            nc.tensor.transpose(out=c_turned[:], in_=c_f32[:], identity=ident[:])
            nc.scalar.copy(out=bias[:], in_=c_turned[:])

        def words(g, side):
            return [x_tiles[part, at][:, i, :].bitcast(F32) for part, at, i in x_places(g, side)]

        def transpose_side(pool, g, side, name):
            xt = pool.tile([P, SLOTS, P], F32, tag=name, name=name)
            for a, view in enumerate(words(g, side)):
                nc.tensor.transpose(out=xt[:, a, :], in_=view, identity=ident[:])
            return xt

        counted = {}
        st = {}
        batch_of = {g: b for b, batch in enumerate(BATCHES) for g in batch}

        def batch_shape(b):
            gi = GRANULES[BATCHES[b][0]][0]
            pieces = half_passes(gi)
            return gi, SLOTS * len(BATCHES[b]) // pieces, pieces

        def count_transpose(g):
            if g < N_G:
                for side in range(2):
                    counted[g, side] = transpose_side(count_ps, g, side, "xc")

        def count(g, side):
            b = batch_of[g]
            gi, bands, pieces = batch_shape(b)
            if g == BATCHES[b][0] and side == 0:
                stats = small.tile([P, bands, pieces, 6], F32)
                st[b, "stats"] = stats
            band = 2 * (GRANULES[g][1] - GRANULES[BATCHES[b][0]][1]) + side
            bank = counted[g, side][:].rearrange("p s m -> p (s m)")
            for h in range(2):
                nc.vector.bn_stats(
                    out=st[b, "stats"][:, band, 2 * GRANULES[g][2] + h, :],
                    in_=bank[:, h * 2 * P : (h + 1) * 2 * P].bitcast(BF16),
                )

        def fields_of(b):
            fields = st[b, "stats"][:].rearrange("p b k (e f) -> p b k e f", f=3)
            return fields[:, :, :, :, 1], fields[:, :, :, :, 2]

        def fold_mean(b):
            gi, bands, pieces = batch_shape(b)
            mean_ps = misc_ps.tile([P, bands * pieces * 2], F32, tag="misc")
            nc.tensor.matmul(
                out=mean_ps[:], lhsT=folds[gi][:].rearrange("p b m -> p (b m)"),
                rhs=fields_of(b)[0].rearrange("p b k e -> p (b k e)"), start=True, stop=True,
            )
            st[b, "mean_ps"] = mean_ps

        def mean_step(b):
            gi, bands, pieces = batch_shape(b)
            neg_mean = small.tile([P, bands, 2], F32)
            nc.vector.tensor_reduce(
                out=neg_mean[:], in_=st[b, "mean_ps"][:].rearrange("p (b k e) -> p b e k", b=bands, e=2),
                axis=AX.X, op=ALU.add, negate=True,
            )
            st[b, "neg_mean"] = neg_mean

        def deviation_step(b):
            gi, bands, pieces = batch_shape(b)
            dev = small.tile([P, bands, pieces, 2], F32)
            nc.vector.tensor_tensor(
                out=dev[:], in0=fields_of(b)[0],
                in1=st[b, "neg_mean"][:].unsqueeze(2).to_broadcast([P, bands, pieces, 2]), op=ALU.add,
            )
            st[b, "dev"] = dev

        def square_step(b):
            gi, bands, pieces = batch_shape(b)
            dev_sq = small.tile([P, bands, pieces, 2], F32)
            nc.vector.tensor_tensor(out=dev_sq[:], in0=st[b, "dev"][:], in1=st[b, "dev"][:], op=ALU.mult)
            st[b, "dev_sq"] = dev_sq

        def spread_step(b):
            gi, bands, pieces = batch_shape(b)
            spread = small.tile([P, bands, pieces, 2], F32)
            nc.vector.scalar_tensor_tensor(
                out=spread[:], in0=fields_of(b)[1], scalar=1.0 / PIECE_COUNT, in1=st[b, "dev_sq"][:],
                op0=ALU.mult, op1=ALU.add,
            )
            st[b, "spread"] = spread

        def fold_var(b):
            gi, bands, pieces = batch_shape(b)
            var_ps = misc_ps.tile([P, bands * pieces * 2], F32, tag="misc")
            nc.tensor.matmul(
                out=var_ps[:], lhsT=folds[gi][:].rearrange("p b m -> p (b m)"),
                rhs=st[b, "spread"][:].rearrange("p b k e -> p (b k e)"), start=True, stop=True,
            )
            st[b, "var_ps"] = var_ps

        def var_step(b):
            gi, bands, pieces = batch_shape(b)
            var = small.tile([P, bands, 2], F32)
            nc.vector.tensor_reduce(
                out=var[:], in_=st[b, "var_ps"][:].rearrange("p (b k e) -> p b e k", b=bands, e=2),
                axis=AX.X, op=ALU.add,
            )
            st[b, "var"] = var

        def std_step(b):
            gi, bands, pieces = batch_shape(b)
            std = small.tile([P, bands, 2], F32)
            nc.scalar.activation(out=std[:], in_=st[b, "var"][:], func=ACT.Sqrt, bias=eps[:])
            st[b, "std"] = std

        def rstd_step(b):
            gi, bands, pieces = batch_shape(b)
            rstd = small.tile([P, bands, 2], F32)
            nc.vector.reciprocal(out=rstd[:], in_=st[b, "std"][:])
            st[b, "rstd"] = rstd

        def offset_step(b):
            gi, bands, pieces = batch_shape(b)
            offset = small.tile([P, bands, 2], F32)
            nc.vector.tensor_tensor(out=offset[:], in0=st[b, "neg_mean"][:], in1=st[b, "rstd"][:], op=ALU.mult)
            st[b, "offset"] = offset

        turned_x = {}
        xhs = {}
        xbs = {}
        ys = {}
        gxs = {}
        gws = {}
        xqs = {}
        wqs = {}

        def norm_transpose(g, side):
            if g < N_G:
                turned_x[g, side] = transpose_side(norm_ps, g, side, "xt")

        def normalise(g, side):
            if g >= N_G:
                return
            b = batch_of[g]
            band = 2 * (GRANULES[g][1] - GRANULES[BATCHES[b][0]][1]) + side
            xh = xh_pool.tile([P, 2, SLOTS, P], F32)
            halves = turned_x[g, side][:].rearrange("p s m -> p (s m)").bitcast(BF16)
            halves = halves.rearrange("p (s w e) -> p s w e", s=SLOTS, e=2)
            for e in range(2):
                nc.scalar.activation(
                    out=xh[:, e, :, :], in_=halves[:, :, :, e], func=ACT.Identity,
                    bias=st[b, "offset"][:, band, e : e + 1], scale=st[b, "rstd"][:, band, e : e + 1],
                )
            xhs[g, side] = xh

        def back_transpose(g, m):
            if g >= N_G:
                return
            xb = back_ps.tile([P, 2, 2, P], F32, tag="xb")
            for side in range(2):
                for e in range(2):
                    nc.tensor.transpose(out=xb[:, side, e, :], in_=xhs[g, side][:, e, m, :], identity=ident[:])
            xbs[g, m] = xb

        def gain_and_shift(g, m):
            gi, pair, quarter = GRANULES[g]
            if m == 0:
                y = y_pool.tile([P, PACK, SLOTS, 2, T], BF16)
                ys[g] = y
            for side in range(2):
                at = GROUP_BASE_PASS[gi] + (2 * pair + side) * 2 * half_passes(gi) + SLOTS * quarter + m
                for j in range(PACK):
                    col = at * PACK + j
                    nc.scalar.activation(
                        out=ys[g][:, j, m, side, :].rearrange("p (e w) -> p e w", e=2),
                        in_=xbs[g, m][:, side, :, 32 * j : 32 * (j + 1)], func=ACT.Identity,
                        bias=shift[:, col : col + 1], scale=gain[:, col : col + 1],
                    )

        def regroup_x(g, first=0, count=SLOTS):
            if first == 0:
                gx = gx_pool.tile([P, SLOTS, 2, PACK * T], BF16, align_bytes=64)
                gxs[g] = gx
            slots = slice(first, first + count)
            nc.vector.tensor_copy(
                out=gxs[g][:, slots, :, :].rearrange("p s a (m i j) -> p (s a m) j i", i=4, j=PACK),
                in_=ys[g][:, :, slots, :, :].rearrange("p j s a (m i) -> p (s a m) j i", i=4),
            )

        def quantise_x(g, first=0, count=SLOTS):
            if first == 0:
                xq = xq_pool.tile([P, SLOTS, 2 * T], U32, align_bytes=64)
                xs = xq_pool.tile([P, SLOTS, 2 * T], U8, align_bytes=64)
                xqs[g] = (xq, xs)
            xq, xs = xqs[g]
            slots = slice(first, first + count)
            nc.vector.quantize_mx(
                out=xq[:, slots, :].rearrange("p s m -> p (s m)").bitcast(FP8X4),
                scales=xs[:, slots, :].rearrange("p s m -> p (s m)"),
                in_=gxs[g][:, slots, :, :].rearrange("p s a m -> p (s a m)"),
            )

        def regroup_w(g, on_gpsimd):
            if g >= N_G:
                return
            if on_gpsimd:
                gw = gw_pool.tile([P, SLOTS, 2, PACK * N_OUT], BF16, align_bytes=64)
                gws[g] = gw
            for side in range(2):
                gi, at, i = w_place(g, side)
                if on_gpsimd:
                    first, last = 0, GPSIMD_W_SLOTS[side]
                else:
                    first, last = GPSIMD_W_SLOTS[side], SLOTS
                if first == last:
                    continue
                grouped = gws[g][:, first:last, side, :]
                rows = w_tiles[gi, at][:, i + first : i + last, :]
                if on_gpsimd:
                    nc.gpsimd.tensor_scalar(
                        out=grouped.rearrange("p c (n j) -> p c n j", j=PACK),
                        in0=rows.rearrange("p c (j n) -> p c n j", j=PACK),
                        scalar1=1.0, scalar2=0.0, op0=ALU.mult, op1=ALU.add,
                    )
                else:
                    nc.vector.tensor_copy(
                        out=grouped.rearrange("p c (m i j) -> p c m j i", i=4, j=PACK),
                        in_=rows.rearrange("p c (j m i) -> p c m j i", j=PACK, i=4),
                    )

        def quantise_w(g):
            wq = wq_pool.tile([P, SLOTS, 2 * N_OUT], U32, align_bytes=64)
            ws = wq_pool.tile([P, SLOTS, 2 * N_OUT], U8, align_bytes=64)
            wqs[g] = (wq, ws)
            nc.vector.quantize_mx(
                out=wq[:].rearrange("p s m -> p (s m)").bitcast(FP8X4),
                scales=ws[:].rearrange("p s m -> p (s m)"),
                in_=gws[g][:].rearrange("p s a m -> p (s a m)"),
            )

        accs = {}

        def quad_pairs(k):
            gi, pair, quarter = GRANULES[k * QUAD]
            per_pair = half_passes(gi) * 2 // SLOTS
            pairs_before = sum((e - s) // (2 * w) for s, e, w in GROUP_BINS[:gi])
            return pairs_before + pair, QUAD // per_pair

        def multiply(k, granules):
            first_pair, pairs = quad_pairs(k)
            per_pair = QUAD // pairs
            if granules[0] == k * QUAD:
                acc = misc_ps.tile([P, pairs, 2 * T], F32, tag="misc")
                accs[k] = acc
            for g in granules:
                wq, ws = wqs[g]
                xq, xs = xqs[g]
                n = g - k * QUAD
                for m in range(SLOTS):
                    nc.tensor.matmul_mx(
                        out=accs[k][:, n // per_pair, :],
                        lhsT=wq[:, m, :].bitcast(FP8X4), lhsT_scale=ws[:, m, :],
                        rhs=xq[:, m, :].bitcast(FP8X4), rhs_scale=xs[:, m, :],
                        start=(n % per_pair == 0 and m == 0),
                        stop=(n % per_pair == per_pair - 1 and m == SLOTS - 1),
                    )

        def add_bias(k):
            first_pair, pairs = quad_pairs(k)
            for pair in range(pairs):
                nc.vector.tensor_scalar(
                    out=result[:, first_pair + pair, :].rearrange("p (a w e) -> p a w e", a=2, e=2),
                    in0=accs[k][:, pair, :].rearrange("p (a e w) -> p a w e", a=2, e=2),
                    scalar1=bias[:, first_pair + pair : first_pair + pair + 1], scalar2=None, op0=ALU.add,
                )

        def store(k):
            first_pair, pairs = quad_pairs(k)
            by_side = out[0].rearrange("n (g a) t -> a n g t", a=2)
            for side in range(2):
                nc.sync.dma_start(
                    out=by_side[side, :, first_pair : first_pair + pairs, :],
                    in_=result[side * N_OUT : (side + 1) * N_OUT, first_pair : first_pair + pairs, side * T : (side + 1) * T],
                )

        count_transpose(0)
        regroup_w(0, True)
        gain_perm = sort_channel_vector(gain_nat, "gain")
        shift_perm = sort_channel_vector(shift_nat, "shift")
        for side in range(2):
            count(0, side)
        count_transpose(1)
        for side in range(2):
            norm_transpose(0, side)
        fold_mean(0)
        count(1, 0)
        mean_step(0)
        deviation_step(0)
        square_step(0)
        spread_step(0)
        fold_var(0)
        turn_channel_vector(gain_perm, gain_cols)
        count(1, 1)
        var_step(0)
        std_step(0)
        count_transpose(2)
        fold_mean(1)
        turn_channel_vector(shift_perm, shift_cols)
        count(2, 0)
        rstd_step(0)
        offset_step(0)
        for side in range(2):
            normalise(0, side)
            norm_transpose(1, side)
        for m in range(2):
            back_transpose(0, m)
        mean_step(1)
        deviation_step(1)
        square_step(1)
        spread_step(1)
        fold_var(1)
        count(2, 1)
        var_step(1)
        std_step(1)
        count_transpose(3)
        fold_mean(2)
        rstd_step(1)
        offset_step(1)
        mean_step(2)
        deviation_step(2)
        square_step(2)
        spread_step(2)
        fold_var(2)

        counted_to = PROLOGUE
        spreading = [2]
        for i in range(N_G):
            load_x(i + X_AHEAD)
            load_w(i + W_AHEAD)
            if i % QUAD == 3 and i >= 7:
                store(i // QUAD - 1)

            fresh = list(range(counted_to, min(i + 1 + min(LEAD, i + 4), N_G)))
            counted_to += len(fresh)
            finished = [b for b, batch in enumerate(BATCHES) if batch[-1] in fresh]

            back_transpose(i, 2)
            normalise(i + 1, 0)
            norm_transpose(i + 2, 0)
            gain_and_shift(i, 0)
            back_transpose(i, 3)
            if fresh:
                count(fresh[0], 0)
            for b in spreading:
                var_step(b)
                std_step(b)
            for g in fresh:
                if g != fresh[0]:
                    count(g, 0)
                count(g, 1)
                count_transpose(g + 1)
            for b in spreading:
                rstd_step(b)
            for b in finished:
                fold_mean(b)
            if i % QUAD == 2 and i >= 6:
                multiply(i // QUAD - 1, list(range(i - 6, i - 2)))
            gain_and_shift(i, 1)
            normalise(i + 1, 1)
            norm_transpose(i + 2, 1)
            gain_and_shift(i, 2)
            back_transpose(i + 1, 0)
            gain_and_shift(i, 3)
            back_transpose(i + 1, 1)

            if i >= 1:
                regroup_x(i - 1)
            for b in spreading:
                offset_step(b)
            for b in finished:
                mean_step(b)
            regroup_w(i, False)
            for b in finished:
                deviation_step(b)
            if i >= 1:
                quantise_x(i - 1)
            for b in finished:
                square_step(b)
            quantise_w(i)
            regroup_w(i + 1, True)
            for b in finished:
                spread_step(b)
                fold_var(b)
            if i % QUAD == 2 and i >= 6:
                add_bias(i // QUAD - 1)
            if i == 2:
                prepare_bias()
            spreading = finished

        last = N_G // QUAD - 1
        multiply(last, list(range(last * QUAD, N_G - 1)))
        for first in (0, 2):
            regroup_x(N_G - 1, first, 2)
        for first in (0, 2):
            quantise_x(N_G - 1, first, 2)
        multiply(last, [N_G - 1])
        add_bias(last)
        store(last)
